import numpy as np
import ml_dtypes


def mxq(x, axis, fmt="e4m3"):
    dtype, down = {"e4m3": (ml_dtypes.float8_e4m3fn, 7), "e5m2": (ml_dtypes.float8_e5m2, 14)}[fmt]
    v = np.moveaxis(np.asarray(x, np.float32).astype(ml_dtypes.bfloat16).astype(np.float64), axis, -1)
    blocks = v.reshape(v.shape[:-1] + (-1, 32))
    amax = np.abs(blocks).max(-1, keepdims=True)
    byte = np.maximum(np.where(amax > 0, np.frexp(amax)[1] - 1 + 127, 0) - down, 1)
    scale = np.exp2(byte - 127.0)
    codes = (blocks / scale).astype(np.float32).astype(dtype).astype(np.float64)
    return np.moveaxis((codes * scale).reshape(v.shape), -1, axis)


WIDE = False


def mx_kscale(k):
    if not WIDE:
        return np.ones(k)
    levels = np.array([10, -10, 5, -5, 0])
    a = np.random.permutation(np.resize(levels, k // 512 * 4)).reshape(k // 512, 4)
    idx = np.arange(k)
    return np.exp2(a[idx // 512, idx % 128 // 32])


BF16 = ml_dtypes.bfloat16


def bf(x):
    return np.asarray(x, np.float32).astype(BF16)


def f64(x):
    return np.asarray(x).astype(np.float64)


N, C_IN, C_OUT, C_DGRAM, C_AA, C_ESM = 128, 512, 128, 39, 22, 1280
LN_EPS = 1e-5


def layer_norm(x, g, b):
    mu = x.mean(-1, keepdims=True)
    var = x.var(-1, keepdims=True)
    return (x - mu) * (1.0 / np.sqrt(var + LN_EPS)) * g + b


def setup_inputs():
    rn, ru = np.random.standard_normal, np.random.uniform
    s = mx_kscale(C_IN)

    def vec():
        return bf(rn(C_OUT) * 0.1)

    def row():
        return bf(rn(C_OUT)[None, :])

    return {
        "act_dgram": bf(rn((N, N, C_OUT)) * 0.2),
        "aa_proj1": bf(rn((N, C_OUT)) * 0.6),
        "aa_proj2": bf(rn((N, C_OUT)) * 0.6),
        "esm_proj1": bf(rn((N, C_OUT))),
        "esm_proj2": bf(rn((N, C_OUT))),
        "query_embedding": bf(rn((N, N, C_IN)) * (0.5 + 1.5 * ru(size=(N, N)))[..., None] + rn((N, N))[..., None]),
        "pseudo_beta_mask": bf(ru(size=N)),
        "backbone_mask": bf(ru(size=N)),
        "multichain_mask_2d": bf(ru(size=(N, N))),
        "unit_x": bf(rn((N, N))),
        "unit_y": bf(rn((N, N))),
        "unit_z": bf(rn((N, N))),
        "ln_g": bf((1.0 + 0.1 * rn(C_IN)) * s),
        "ln_b": bf(0.1 * rn(C_IN) * s),
        "w_q": bf(rn((C_IN, C_OUT)) / np.sqrt(C_IN) / s[:, None]),
        "b_q": vec(),
        "w_pbm": row(), "b_pbm": vec(),
        "w_x": row(), "b_x": vec(),
        "w_y": row(), "b_y": vec(),
        "w_z": row(), "b_z": vec(),
        "w_bb": row(), "b_bb": vec(),
    }


def reference(act_dgram, aa_proj1, aa_proj2, esm_proj1, esm_proj2, query_embedding,
              pseudo_beta_mask, backbone_mask, multichain_mask_2d, unit_x, unit_y, unit_z,
              ln_g, ln_b, w_q, b_q, w_pbm, b_pbm, w_x, b_x, w_y, b_y, w_z, b_z, w_bb, b_bb):
    pbm, bbm, mc = f64(pseudo_beta_mask), f64(backbone_mask), f64(multichain_mask_2d)
    pb2 = pbm[:, None] * pbm[None, :] * mc
    bb2 = bbm[:, None] * bbm[None, :] * mc
    act = f64(act_dgram)
    act = act + (pb2[..., None] * f64(w_pbm)[0] + f64(b_pbm))
    act = act + f64(aa_proj1)[None, :, :]
    act = act + f64(aa_proj2)[:, None, :]
    act = act + ((f64(unit_x) * bb2)[..., None] * f64(w_x)[0] + f64(b_x))
    act = act + ((f64(unit_y) * bb2)[..., None] * f64(w_y)[0] + f64(b_y))
    act = act + ((f64(unit_z) * bb2)[..., None] * f64(w_z)[0] + f64(b_z))
    act = act + (bb2[..., None] * f64(w_bb)[0] + f64(b_bb))
    act = act + f64(esm_proj1)[None, :, :]
    act = act + f64(esm_proj2)[:, None, :]
    q = layer_norm(f64(query_embedding), f64(ln_g), f64(ln_b))
    act = act + (mxq(q, 2, "e4m3") @ mxq(f64(w_q), 0, "e4m3")) + f64(b_q)
    return act

@@ -1,0 +1,220 @@
+from contextlib import ExitStack
+
+import concourse.bass as bass
+import concourse.mybir as mybir
+import concourse.tile as tile
+from concourse.masks import make_identity
+
+F32 = mybir.dt.float32
+BF16 = mybir.dt.bfloat16
+U32 = mybir.dt.uint32
+U8 = mybir.dt.uint8
+FP8X4 = mybir.dt.float8_e4m3fn_x4
+ALU = mybir.AluOpType
+ACT = mybir.ActivationFunctionType
+
+P = 128
+C_IN = 512
+PACK = 4
+LN_EPS = 1e-5
+GROUP = 4
+N_GROUPS = P // GROUP
+N_FEAT = 5
+LOAD_AHEAD = 3
+
+ROW_GAIN = 0
+ROW_SHIFT = 4
+ROW_BIAS = 8
+ROW_W = 14
+ROW_PBM = 19
+ROW_BBM = 20
+N_ROWS = 21
+
+FLOPS = 2 * P * P * C_IN * P
+
+
+def as_row(vector):
+    return vector.rearrange("(o c) -> o c", o=1)
+
+
+def tile_templatepairembeddermultimer_pa_kernel(
+    tc,
+    act_dgram, aa_proj1, aa_proj2, esm_proj1, esm_proj2, query_embedding,
+    pseudo_beta_mask, backbone_mask, multichain_mask_2d, unit_x, unit_y, unit_z,
+    ln_g, ln_b, w_q, b_q, w_pbm, b_pbm, w_x, b_x, w_y, b_y, w_z, b_z, w_bb, b_bb,
+    out,
+):
+    nc = tc.nc
+    with ExitStack() as stack:
+        keep = stack.enter_context(tc.tile_pool(name="keep", bufs=1))
+        x_pool = stack.enter_context(tc.tile_pool(name="x", bufs=LOAD_AHEAD + 2))
+        act_pool = stack.enter_context(tc.tile_pool(name="act", bufs=LOAD_AHEAD + 3))
+        stat_pool = stack.enter_context(tc.tile_pool(name="stat", bufs=4))
+        work = stack.enter_context(tc.tile_pool(name="work", bufs=3))
+        psum_keep = stack.enter_context(tc.psum_pool(name="psum_keep", bufs=1))
+
+        x_tiles = {}
+        act_tiles = {}
+
+        def load(g):
+            cols = slice(g * GROUP, (g + 1) * GROUP)
+            x_g = x_pool.tile([P, GROUP, C_IN], BF16, name="x_g")
+            nc.sync.dma_start(out=x_g[:], in_=query_embedding[:, cols, :])
+            act_g = act_pool.tile([P, GROUP, P], BF16, name="act_g")
+            nc.sync.dma_start(out=act_g[:], in_=act_dgram[:, cols, :])
+            x_tiles[g] = x_g
+            act_tiles[g] = act_g
+
+        for g in range(LOAD_AHEAD):
+            load(g)
+
+        ident_f = keep.tile([P, P], F32, name="ident_f")
+        make_identity(nc, ident_f[:])
+        ident_b = keep.tile([P, P], BF16, name="ident_b")
+        make_identity(nc, ident_b[:])
+        eps = keep.tile([P, 1], F32, name="eps")
+        nc.vector.memset(eps[:], LN_EPS)
+
+        rows = keep.tile([P, P], BF16, name="rows")
+        nc.vector.memset(rows[:], 0.0)
+        nc.scalar.dma_start(out=rows[ROW_GAIN : ROW_GAIN + PACK, :], in_=ln_g.rearrange("(t p) -> t p", p=P))
+        nc.scalar.dma_start(out=rows[ROW_SHIFT : ROW_SHIFT + PACK, :], in_=ln_b.rearrange("(t p) -> t p", p=P))
+        for n, vector in enumerate((b_q, b_pbm, b_x, b_y, b_z, b_bb)):
+            nc.scalar.dma_start(out=rows[ROW_BIAS + n : ROW_BIAS + n + 1, :], in_=as_row(vector))
+        for n, row in enumerate((w_pbm, w_x, w_y, w_z, w_bb)):
+            nc.scalar.dma_start(out=rows[ROW_W + n : ROW_W + n + 1, :], in_=row)
+        nc.scalar.dma_start(out=rows[ROW_PBM : ROW_PBM + 1, :], in_=as_row(pseudo_beta_mask))
+        nc.scalar.dma_start(out=rows[ROW_BBM : ROW_BBM + 1, :], in_=as_row(backbone_mask))
+
+        small = {}
+        for name, matrix in (
+            ("mc", multichain_mask_2d), ("ux", unit_x), ("uy", unit_y), ("uz", unit_z),
+            ("aa1", aa_proj1), ("esm1", esm_proj1), ("aa2", aa_proj2), ("esm2", esm_proj2),
+        ):
+            small[name] = keep.tile([P, P], BF16, name="in_" + name)
+            nc.gpsimd.dma_start(out=small[name][:], in_=matrix)
+        w_planes = keep.tile([P, PACK, P], BF16, name="w_planes")
+        nc.gpsimd.dma_start(out=w_planes[:], in_=w_q.rearrange("(t p) c -> p t c", p=P))
+
+        cols = keep.tile([P, N_ROWS], F32, name="cols")
+        bias_total = keep.tile([P, 1], F32, name="bias_total")
+        row_term_t = keep.tile([P, P], F32, name="row_term_t")
+        col_term_t = keep.tile([P, P], F32, name="col_term_t")
+        feat = keep.tile([P, N_FEAT, P], F32, name="feat")
+        spread_a = psum_keep.tile([P, 4, P], F32, name="spread_a")
+        spread_b = psum_keep.tile([P, 3, P], F32, name="spread_b")
+
+        def spread(dst, column):
+            nc.tensor.transpose(dst, cols[:, column : column + 1].to_broadcast([P, P]), ident_f[:])
+
+        with tc.psum_pool(name="psum_setup", bufs=1) as psum_setup:
+            rows_t = psum_setup.tile([P, P], BF16, name="rows_t")
+            nc.tensor.transpose(rows_t[:], rows[:], ident_b[:])
+            nc.vector.tensor_copy(out=cols[:], in_=rows_t[:, 0:N_ROWS])
+            nc.vector.reduce_sum(out=bias_total[:], in_=cols[:, ROW_BIAS : ROW_BIAS + 6], axis=mybir.AxisListType.X)
+            for m in range(4):
+                spread(spread_a[:, m, :], ROW_W + m)
+            spread(spread_b[:, 0, :], ROW_W + 4)
+            spread(spread_b[:, 1, :], ROW_PBM)
+            spread(spread_b[:, 2, :], ROW_BBM)
+
+            row_term = keep.tile([P, P], F32, name="row_term")
+            nc.vector.tensor_tensor(out=row_term[:], in0=small["aa1"][:], in1=small["esm1"][:], op=ALU.add)
+            col_term = keep.tile([P, P], F32, name="col_term")
+            nc.vector.tensor_tensor(out=col_term[:], in0=small["aa2"][:], in1=small["esm2"][:], op=ALU.add)
+            row_ps = psum_setup.tile([P, P], F32, name="row_ps")
+            nc.tensor.transpose(row_ps[:], row_term[:], ident_f[:])
+            nc.vector.tensor_copy(out=row_term_t[:], in_=row_ps[:])
+            col_ps = psum_setup.tile([P, P], F32, name="col_ps")
+            nc.tensor.transpose(col_ps[:], col_term[:], ident_f[:])
+            nc.vector.tensor_scalar(out=col_term_t[:], in0=col_ps[:], scalar1=bias_total[:, 0:1], scalar2=None, op0=ALU.add)
+
+        w_spread = [spread_a[:, m, :] for m in range(4)] + [spread_b[:, 0, :]]
+
+        nc.vector.scalar_tensor_tensor(
+            out=feat[:, 0, :], in0=small["mc"][:], scalar=cols[:, ROW_PBM : ROW_PBM + 1], in1=spread_b[:, 1, :],
+            op0=ALU.mult, op1=ALU.mult)
+        nc.vector.scalar_tensor_tensor(
+            out=feat[:, 4, :], in0=small["mc"][:], scalar=cols[:, ROW_BBM : ROW_BBM + 1], in1=spread_b[:, 2, :],
+            op0=ALU.mult, op1=ALU.mult)
+        for m, name in ((1, "ux"), (2, "uy"), (3, "uz")):
+            nc.vector.tensor_tensor(out=feat[:, m, :], in0=small[name][:], in1=feat[:, 4, :], op=ALU.mult)
+
+        w_grouped = keep.tile([P, P, PACK], BF16, name="w_grouped", align_bytes=64)
+        nc.vector.tensor_copy(out=w_grouped[:], in_=w_planes[:].rearrange("p t c -> p c t"))
+        w_codes = keep.tile([P, P], U32, name="w_codes", align_bytes=64)
+        w_scales = keep.tile([P, P], U8, name="w_scales", align_bytes=64)
+        nc.vector.quantize_mx(
+            out=w_codes[:].bitcast(FP8X4), scales=w_scales[:], in_=w_grouped[:].rearrange("p c t -> p (c t)"))
+
+        psum_y = stack.enter_context(tc.psum_pool(name="psum_y", bufs=3))
+        psum_mx = stack.enter_context(tc.psum_pool(name="psum_mx", bufs=2))
+        psum_base = stack.enter_context(tc.psum_pool(name="psum_base", bufs=1))
+
+        for g in range(N_GROUPS):
+            if g + LOAD_AHEAD < N_GROUPS:
+                load(g + LOAD_AHEAD)
+            x_g = x_tiles.pop(g)
+            act_g = act_tiles.pop(g)
+
+            stats = stat_pool.tile([P, GROUP, 6], F32, name="stats")
+            mean_var = stat_pool.tile([P, GROUP, 2], F32, name="mean_var")
+            for jj in range(GROUP):
+                nc.vector.bn_stats(out=stats[:, jj, :], in_=x_g[:, jj, :])
+                nc.vector.bn_aggr(out=mean_var[:, jj, :], in_=stats[:, jj, :])
+            std = stat_pool.tile([P, GROUP], F32, name="std")
+            nc.scalar.activation(out=std[:], in_=mean_var[:, :, 1], func=ACT.Sqrt, bias=eps[:, 0:1], scale=1.0)
+            rstd = stat_pool.tile([P, GROUP], F32, name="rstd")
+            nc.vector.reciprocal(out=rstd[:], in_=std[:])
+            neg_mean = stat_pool.tile([P, GROUP], F32, name="neg_mean")
+            nc.vector.tensor_scalar(out=neg_mean[:], in0=mean_var[:, :, 0], scalar1=-1.0, scalar2=None, op0=ALU.mult)
+
+            y_g = work.tile([P, GROUP, C_IN], F32, name="y_g")
+            for jj in range(GROUP):
+                nc.gpsimd.tensor_scalar(
+                    out=y_g[:, jj, :], in0=x_g[:, jj, :],
+                    scalar1=neg_mean[:, jj : jj + 1], scalar2=rstd[:, jj : jj + 1], op0=ALU.add, op1=ALU.mult)
+
+            q_planes = work.tile([P, PACK, GROUP * P], BF16, name="q_planes")
+            for t in range(PACK):
+                y_t = psum_y.tile([P, GROUP, P], F32, name="y_t")
+                for jj in range(GROUP):
+                    nc.tensor.transpose(y_t[:, jj, :], y_g[:, jj, t * P : (t + 1) * P], ident_f[:])
+                nc.scalar.activation(
+                    out=q_planes[:, t, :], in_=y_t[:].rearrange("p a b -> p (a b)"), func=ACT.Identity,
+                    scale=cols[:, ROW_GAIN + t : ROW_GAIN + t + 1], bias=cols[:, ROW_SHIFT + t : ROW_SHIFT + t + 1])
+
+            q_grouped = work.tile([P, GROUP * P, PACK], BF16, name="q_grouped", align_bytes=64)
+            nc.scalar.copy(out=q_grouped[:], in_=q_planes[:].rearrange("p t r -> p r t"))
+            q_codes = work.tile([P, GROUP * P], U32, name="q_codes", align_bytes=64)
+            q_scales = work.tile([P, GROUP * P], U8, name="q_scales", align_bytes=64)
+            nc.vector.quantize_mx(
+                out=q_codes[:].bitcast(FP8X4), scales=q_scales[:], in_=q_grouped[:].rearrange("p r t -> p (r t)"))
+
+            proj = psum_mx.tile([P, GROUP, P], F32, name="proj")
+            for jj in range(GROUP):
+                pairs = slice(jj * P, (jj + 1) * P)
+                nc.tensor.matmul_mx(
+                    out=proj[:, jj, :],
+                    lhsT=q_codes[:, pairs].bitcast(FP8X4), lhsT_scale=q_scales[:, pairs],
+                    rhs=w_codes[:].bitcast(FP8X4), rhs_scale=w_scales[:],
+                    start=True, stop=True)
+
+            base = psum_base.tile([P, GROUP, P], F32, name="base")
+            for jj in range(GROUP):
+                j = g * GROUP + jj
+                nc.tensor.matmul(out=base[:, jj, :], lhsT=col_term_t[:], rhs=ident_f[:], is_transpose=True,
+                                 start=True, stop=False)
+                nc.tensor.matmul(out=base[:, jj, :], lhsT=row_term_t[:, j : j + 1].to_broadcast([P, P]), rhs=ident_f[:],
+                                 is_transpose=True, start=False, stop=True)
+
+            res = work.tile([P, GROUP, P], F32, name="res")
+            for m in range(N_FEAT):
+                for jj in range(GROUP):
+                    j = g * GROUP + jj
+                    nc.vector.scalar_tensor_tensor(
+                        out=res[:, jj, :], in0=w_spread[m], scalar=feat[:, m, j : j + 1],
+                        in1=act_g[:, jj, :] if m == 0 else res[:, jj, :], op0=ALU.mult, op1=ALU.add)
+            nc.vector.tensor_tensor(out=res[:], in0=res[:], in1=base[:], op=ALU.add)
+            nc.vector.tensor_tensor(out=res[:], in0=res[:], in1=proj[:], op=ALU.add)
+            nc.sync.dma_start(out=out[:, g * GROUP : (g + 1) * GROUP, :], in_=res[:])

@@ -1,8 +1,6 @@
 from contextlib import ExitStack
 
-import concourse.bass as bass
 import concourse.mybir as mybir
-import concourse.tile as tile
 from concourse.masks import make_identity
 
 F32 = mybir.dt.float32
@@ -22,14 +20,6 @@ N_GROUPS = P // GROUP
 N_FEAT = 5
 LOAD_AHEAD = 3
 
-ROW_GAIN = 0
-ROW_SHIFT = 4
-ROW_BIAS = 8
-ROW_W = 14
-ROW_PBM = 19
-ROW_BBM = 20
-N_ROWS = 21
-
 FLOPS = 2 * P * P * C_IN * P
 
 
@@ -47,134 +37,70 @@ def tile_templatepairembeddermultimer_pa_kernel(
     nc = tc.nc
     with ExitStack() as stack:
         keep = stack.enter_context(tc.tile_pool(name="keep", bufs=1))
-        x_pool = stack.enter_context(tc.tile_pool(name="x", bufs=LOAD_AHEAD + 2))
-        act_pool = stack.enter_context(tc.tile_pool(name="act", bufs=LOAD_AHEAD + 3))
-        stat_pool = stack.enter_context(tc.tile_pool(name="stat", bufs=4))
-        work = stack.enter_context(tc.tile_pool(name="work", bufs=3))
+        x_pool = stack.enter_context(tc.tile_pool(name="x", bufs=LOAD_AHEAD + 3))
+        act_pool = stack.enter_context(tc.tile_pool(name="act", bufs=LOAD_AHEAD + 4))
+        stat_pool = stack.enter_context(tc.tile_pool(name="stat", bufs=6))
+        work = stack.enter_context(tc.tile_pool(name="work", bufs=4))
+        scrap = stack.enter_context(tc.tile_pool(name="scrap", bufs=4))
         psum_keep = stack.enter_context(tc.psum_pool(name="psum_keep", bufs=1))
+        psum_y = stack.enter_context(tc.psum_pool(name="psum_y", bufs=3))
 
         x_tiles = {}
         act_tiles = {}
+        y_tiles = {}
+        code_tiles = {}
 
         def load(g):
-            cols = slice(g * GROUP, (g + 1) * GROUP)
-            x_g = x_pool.tile([P, GROUP, C_IN], BF16, name="x_g")
-            nc.sync.dma_start(out=x_g[:], in_=query_embedding[:, cols, :])
-            act_g = act_pool.tile([P, GROUP, P], BF16, name="act_g")
-            nc.sync.dma_start(out=act_g[:], in_=act_dgram[:, cols, :])
-            x_tiles[g] = x_g
-            act_tiles[g] = act_g
+            columns = slice(g * GROUP, (g + 1) * GROUP)
+            x_tiles[g] = x_pool.tile([P, GROUP, C_IN], BF16, name="x_g")
+            nc.sync.dma_start(out=x_tiles[g][:], in_=query_embedding[:, columns, :])
+            act_tiles[g] = act_pool.tile([P, GROUP, P], BF16, name="act_g")
+            nc.sync.dma_start(out=act_tiles[g][:], in_=act_dgram[:, columns, :])
 
-        for g in range(LOAD_AHEAD):
-            load(g)
+        def load_rows(name, vectors):
+            rows = keep.tile([P, P], BF16, name=name)
+            nc.vector.memset(rows[:], 0.0)
+            first = 0
+            for vector in vectors:
+                n = vector.shape[0]
+                nc.sync.dma_start(out=rows[first : first + n, :], in_=vector)
+                first += n
+            return rows
 
-        ident_f = keep.tile([P, P], F32, name="ident_f")
-        make_identity(nc, ident_f[:])
-        ident_b = keep.tile([P, P], BF16, name="ident_b")
-        make_identity(nc, ident_b[:])
-        eps = keep.tile([P, 1], F32, name="eps")
-        nc.vector.memset(eps[:], LN_EPS)
+        def rows_to_columns(name, rows, n_rows, bank):
+            nc.tensor.transpose(bank, rows[:], ident_b[:])
+            columns = keep.tile([P, n_rows], F32, name=name)
+            nc.vector.tensor_copy(out=columns[:], in_=bank[:, 0:n_rows])
+            return columns
 
-        rows = keep.tile([P, P], BF16, name="rows")
-        nc.vector.memset(rows[:], 0.0)
-        nc.scalar.dma_start(out=rows[ROW_GAIN : ROW_GAIN + PACK, :], in_=ln_g.rearrange("(t p) -> t p", p=P))
-        nc.scalar.dma_start(out=rows[ROW_SHIFT : ROW_SHIFT + PACK, :], in_=ln_b.rearrange("(t p) -> t p", p=P))
-        for n, vector in enumerate((b_q, b_pbm, b_x, b_y, b_z, b_bb)):
-            nc.scalar.dma_start(out=rows[ROW_BIAS + n : ROW_BIAS + n + 1, :], in_=as_row(vector))
-        for n, row in enumerate((w_pbm, w_x, w_y, w_z, w_bb)):
-            nc.scalar.dma_start(out=rows[ROW_W + n : ROW_W + n + 1, :], in_=row)
-        nc.scalar.dma_start(out=rows[ROW_PBM : ROW_PBM + 1, :], in_=as_row(pseudo_beta_mask))
-        nc.scalar.dma_start(out=rows[ROW_BBM : ROW_BBM + 1, :], in_=as_row(backbone_mask))
-
-        small = {}
-        for name, matrix in (
-            ("mc", multichain_mask_2d), ("ux", unit_x), ("uy", unit_y), ("uz", unit_z),
-            ("aa1", aa_proj1), ("esm1", esm_proj1), ("aa2", aa_proj2), ("esm2", esm_proj2),
-        ):
-            small[name] = keep.tile([P, P], BF16, name="in_" + name)
-            nc.gpsimd.dma_start(out=small[name][:], in_=matrix)
-        w_planes = keep.tile([P, PACK, P], BF16, name="w_planes")
-        nc.gpsimd.dma_start(out=w_planes[:], in_=w_q.rearrange("(t p) c -> p t c", p=P))
-
-        cols = keep.tile([P, N_ROWS], F32, name="cols")
-        bias_total = keep.tile([P, 1], F32, name="bias_total")
-        row_term_t = keep.tile([P, P], F32, name="row_term_t")
-        col_term_t = keep.tile([P, P], F32, name="col_term_t")
-        feat = keep.tile([P, N_FEAT, P], F32, name="feat")
-        spread_a = psum_keep.tile([P, 4, P], F32, name="spread_a")
-        spread_b = psum_keep.tile([P, 3, P], F32, name="spread_b")
-
-        def spread(dst, column):
-            nc.tensor.transpose(dst, cols[:, column : column + 1].to_broadcast([P, P]), ident_f[:])
-
-        with tc.psum_pool(name="psum_setup", bufs=1) as psum_setup:
-            rows_t = psum_setup.tile([P, P], BF16, name="rows_t")
-            nc.tensor.transpose(rows_t[:], rows[:], ident_b[:])
-            nc.vector.tensor_copy(out=cols[:], in_=rows_t[:, 0:N_ROWS])
-            nc.vector.reduce_sum(out=bias_total[:], in_=cols[:, ROW_BIAS : ROW_BIAS + 6], axis=mybir.AxisListType.X)
-            for m in range(4):
-                spread(spread_a[:, m, :], ROW_W + m)
-            spread(spread_b[:, 0, :], ROW_W + 4)
-            spread(spread_b[:, 1, :], ROW_PBM)
-            spread(spread_b[:, 2, :], ROW_BBM)
-
-            row_term = keep.tile([P, P], F32, name="row_term")
-            nc.vector.tensor_tensor(out=row_term[:], in0=small["aa1"][:], in1=small["esm1"][:], op=ALU.add)
-            col_term = keep.tile([P, P], F32, name="col_term")
-            nc.vector.tensor_tensor(out=col_term[:], in0=small["aa2"][:], in1=small["esm2"][:], op=ALU.add)
-            row_ps = psum_setup.tile([P, P], F32, name="row_ps")
-            nc.tensor.transpose(row_ps[:], row_term[:], ident_f[:])
-            nc.vector.tensor_copy(out=row_term_t[:], in_=row_ps[:])
-            col_ps = psum_setup.tile([P, P], F32, name="col_ps")
-            nc.tensor.transpose(col_ps[:], col_term[:], ident_f[:])
-            nc.vector.tensor_scalar(out=col_term_t[:], in0=col_ps[:], scalar1=bias_total[:, 0:1], scalar2=None, op0=ALU.add)
-
-        w_spread = [spread_a[:, m, :] for m in range(4)] + [spread_b[:, 0, :]]
-
-        nc.vector.scalar_tensor_tensor(
-            out=feat[:, 0, :], in0=small["mc"][:], scalar=cols[:, ROW_PBM : ROW_PBM + 1], in1=spread_b[:, 1, :],
-            op0=ALU.mult, op1=ALU.mult)
-        nc.vector.scalar_tensor_tensor(
-            out=feat[:, 4, :], in0=small["mc"][:], scalar=cols[:, ROW_BBM : ROW_BBM + 1], in1=spread_b[:, 2, :],
-            op0=ALU.mult, op1=ALU.mult)
-        for m, name in ((1, "ux"), (2, "uy"), (3, "uz")):
-            nc.vector.tensor_tensor(out=feat[:, m, :], in0=small[name][:], in1=feat[:, 4, :], op=ALU.mult)
-
-        w_grouped = keep.tile([P, P, PACK], BF16, name="w_grouped", align_bytes=64)
-        nc.vector.tensor_copy(out=w_grouped[:], in_=w_planes[:].rearrange("p t c -> p c t"))
-        w_codes = keep.tile([P, P], U32, name="w_codes", align_bytes=64)
-        w_scales = keep.tile([P, P], U8, name="w_scales", align_bytes=64)
-        nc.vector.quantize_mx(
-            out=w_codes[:].bitcast(FP8X4), scales=w_scales[:], in_=w_grouped[:].rearrange("p c t -> p (c t)"))
-
-        psum_y = stack.enter_context(tc.psum_pool(name="psum_y", bufs=3))
-        psum_mx = stack.enter_context(tc.psum_pool(name="psum_mx", bufs=2))
-        psum_base = stack.enter_context(tc.psum_pool(name="psum_base", bufs=1))
-
-        for g in range(N_GROUPS):
-            if g + LOAD_AHEAD < N_GROUPS:
-                load(g + LOAD_AHEAD)
-            x_g = x_tiles.pop(g)
-            act_g = act_tiles.pop(g)
-
-            stats = stat_pool.tile([P, GROUP, 6], F32, name="stats")
-            mean_var = stat_pool.tile([P, GROUP, 2], F32, name="mean_var")
+        def normalise(g):
+            x_g = x_tiles[g]
+            row_sum = stat_pool.tile([P, GROUP], F32, name="row_sum")
             for jj in range(GROUP):
-                nc.vector.bn_stats(out=stats[:, jj, :], in_=x_g[:, jj, :])
-                nc.vector.bn_aggr(out=mean_var[:, jj, :], in_=stats[:, jj, :])
+                unread_v = scrap.tile([P, C_IN], BF16, name="unread_v")
+                nc.vector.tensor_scalar(
+                    out=unread_v[:], in0=x_g[:, jj, :], scalar1=1.0, scalar2=None, op0=ALU.mult, op1=ALU.add,
+                    accum_out=row_sum[:, jj : jj + 1])
+            neg_mean = stat_pool.tile([P, GROUP], F32, name="neg_mean")
+            nc.vector.tensor_scalar(out=neg_mean[:], in0=row_sum[:], scalar1=-1.0 / C_IN, scalar2=None, op0=ALU.mult)
+            dev_sq = stat_pool.tile([P, GROUP], F32, name="dev_sq")
+            for jj in range(GROUP):
+                unread_s = scrap.tile([P, C_IN], BF16, name="unread_s")
+                nc.scalar.activation(
+                    out=unread_s[:], in_=x_g[:, jj, :], func=ACT.Square, bias=neg_mean[:, jj : jj + 1], scale=1.0,
+                    accum_out=dev_sq[:, jj : jj + 1])
             std = stat_pool.tile([P, GROUP], F32, name="std")
-            nc.scalar.activation(out=std[:], in_=mean_var[:, :, 1], func=ACT.Sqrt, bias=eps[:, 0:1], scale=1.0)
+            nc.scalar.activation(out=std[:], in_=dev_sq[:], func=ACT.Sqrt, bias=eps[:, 0:1], scale=1.0 / C_IN)
             rstd = stat_pool.tile([P, GROUP], F32, name="rstd")
             nc.vector.reciprocal(out=rstd[:], in_=std[:])
-            neg_mean = stat_pool.tile([P, GROUP], F32, name="neg_mean")
-            nc.vector.tensor_scalar(out=neg_mean[:], in0=mean_var[:, :, 0], scalar1=-1.0, scalar2=None, op0=ALU.mult)
-
-            y_g = work.tile([P, GROUP, C_IN], F32, name="y_g")
+            y_tiles[g] = work.tile([P, GROUP, C_IN], F32, name="y_g")
             for jj in range(GROUP):
                 nc.gpsimd.tensor_scalar(
-                    out=y_g[:, jj, :], in0=x_g[:, jj, :],
+                    out=y_tiles[g][:, jj, :], in0=x_g[:, jj, :],
                     scalar1=neg_mean[:, jj : jj + 1], scalar2=rstd[:, jj : jj + 1], op0=ALU.add, op1=ALU.mult)
 
+        def quantise(g):
+            y_g = y_tiles[g]
             q_planes = work.tile([P, PACK, GROUP * P], BF16, name="q_planes")
             for t in range(PACK):
                 y_t = psum_y.tile([P, GROUP, P], F32, name="y_t")
@@ -182,32 +108,37 @@ def tile_templatepairembeddermultimer_pa_kernel(
                     nc.tensor.transpose(y_t[:, jj, :], y_g[:, jj, t * P : (t + 1) * P], ident_f[:])
                 nc.scalar.activation(
                     out=q_planes[:, t, :], in_=y_t[:].rearrange("p a b -> p (a b)"), func=ACT.Identity,
-                    scale=cols[:, ROW_GAIN + t : ROW_GAIN + t + 1], bias=cols[:, ROW_SHIFT + t : ROW_SHIFT + t + 1])
-
+                    scale=ln_columns[:, t : t + 1], bias=ln_columns[:, PACK + t : PACK + t + 1])
             q_grouped = work.tile([P, GROUP * P, PACK], BF16, name="q_grouped", align_bytes=64)
-            nc.scalar.copy(out=q_grouped[:], in_=q_planes[:].rearrange("p t r -> p r t"))
+            nc.gpsimd.tensor_scalar(
+                out=q_grouped[:], in0=q_planes[:].rearrange("p t r -> p r t"), scalar1=1.0, scalar2=0.0,
+                op0=ALU.mult, op1=ALU.add)
             q_codes = work.tile([P, GROUP * P], U32, name="q_codes", align_bytes=64)
             q_scales = work.tile([P, GROUP * P], U8, name="q_scales", align_bytes=64)
             nc.vector.quantize_mx(
                 out=q_codes[:].bitcast(FP8X4), scales=q_scales[:], in_=q_grouped[:].rearrange("p r t -> p (r t)"))
+            code_tiles[g] = (q_codes, q_scales)
 
-            proj = psum_mx.tile([P, GROUP, P], F32, name="proj")
-            for jj in range(GROUP):
-                pairs = slice(jj * P, (jj + 1) * P)
-                nc.tensor.matmul_mx(
-                    out=proj[:, jj, :],
-                    lhsT=q_codes[:, pairs].bitcast(FP8X4), lhsT_scale=q_scales[:, pairs],
-                    rhs=w_codes[:].bitcast(FP8X4), rhs_scale=w_scales[:],
-                    start=True, stop=True)
-
+        def finish(g):
+            q_codes, q_scales = code_tiles[g]
+            act_g = act_tiles[g]
+            proj_ps = psum_mx.tile([P, GROUP * P], F32, name="proj_ps")
+            nc.tensor.matmul_mx(
+                out=proj_ps[:],
+                lhsT=w_codes[:].bitcast(FP8X4), lhsT_scale=w_scales[:],
+                rhs=q_codes[:].bitcast(FP8X4), rhs_scale=q_scales[:],
+                start=True, stop=True)
+            proj_t = work.tile([P, GROUP, P], F32, name="proj_t")
+            nc.scalar.copy(out=proj_t[:].rearrange("p a b -> p (a b)"), in_=proj_ps[:])
             base = psum_base.tile([P, GROUP, P], F32, name="base")
             for jj in range(GROUP):
                 j = g * GROUP + jj
                 nc.tensor.matmul(out=base[:, jj, :], lhsT=col_term_t[:], rhs=ident_f[:], is_transpose=True,
                                  start=True, stop=False)
                 nc.tensor.matmul(out=base[:, jj, :], lhsT=row_term_t[:, j : j + 1].to_broadcast([P, P]), rhs=ident_f[:],
-                                 is_transpose=True, start=False, stop=True)
-
+                                 is_transpose=True, start=False, stop=False)
+                nc.tensor.matmul(out=base[:, jj, :], lhsT=proj_t[:, jj, :], rhs=ident_f[:], is_transpose=True,
+                                 start=False, stop=True)
             res = work.tile([P, GROUP, P], F32, name="res")
             for m in range(N_FEAT):
                 for jj in range(GROUP):
@@ -216,5 +147,100 @@ def tile_templatepairembeddermultimer_pa_kernel(
                         out=res[:, jj, :], in0=w_spread[m], scalar=feat[:, m, j : j + 1],
                         in1=act_g[:, jj, :] if m == 0 else res[:, jj, :], op0=ALU.mult, op1=ALU.add)
             nc.vector.tensor_tensor(out=res[:], in0=res[:], in1=base[:], op=ALU.add)
-            nc.vector.tensor_tensor(out=res[:], in0=res[:], in1=proj[:], op=ALU.add)
             nc.sync.dma_start(out=out[:, g * GROUP : (g + 1) * GROUP, :], in_=res[:])
+
+        load(0)
+        eps = keep.tile([P, 1], F32, name="eps")
+        nc.vector.memset(eps[:], LN_EPS)
+        table_warm = keep.tile([P, 1], F32, name="table_warm")
+        nc.scalar.activation(out=table_warm[:], in_=eps[:], func=ACT.Sqrt)
+        ident_f = keep.tile([P, P], F32, name="ident_f")
+        make_identity(nc, ident_f[:])
+        ident_b = keep.tile([P, P], BF16, name="ident_b")
+        make_identity(nc, ident_b[:])
+
+        ln_rows = load_rows("ln_rows", (ln_g.rearrange("(t p) -> t p", p=P), ln_b.rearrange("(t p) -> t p", p=P)))
+        w_planes = keep.tile([P, PACK, P], BF16, name="w_planes")
+        nc.sync.dma_start(out=w_planes[:], in_=w_q.rearrange("(t p) c -> p t c", p=P))
+        load(1)
+        pair_rows = load_rows(
+            "pair_rows", (w_pbm, w_x, w_y, w_z, w_bb, as_row(pseudo_beta_mask), as_row(backbone_mask),
+                          as_row(b_q), as_row(b_pbm), as_row(b_x), as_row(b_y), as_row(b_z), as_row(b_bb)))
+        COL_PBM, COL_BBM, COL_BIAS, N_PAIR_COLS = 5, 6, 7, 13
+        small = {}
+        for name, matrix in (
+            ("mc", multichain_mask_2d), ("ux", unit_x), ("uy", unit_y), ("uz", unit_z),
+            ("aa1", aa_proj1), ("esm1", esm_proj1), ("aa2", aa_proj2), ("esm2", esm_proj2),
+        ):
+            small[name] = keep.tile([P, P], BF16, name="in_" + name)
+            nc.sync.dma_start(out=small[name][:], in_=matrix)
+        load(2)
+
+        normalise(0)
+        normalise(1)
+
+        bias_total = keep.tile([P, 1], F32, name="bias_total")
+        row_term_t = keep.tile([P, P], F32, name="row_term_t")
+        col_term_t = keep.tile([P, P], F32, name="col_term_t")
+        feat = keep.tile([P, N_FEAT, P], F32, name="feat")
+        spread_a = psum_keep.tile([P, 4, P], F32, name="spread_a")
+        spread_b = psum_keep.tile([P, 3, P], F32, name="spread_b")
+
+        with tc.psum_pool(name="psum_setup", bufs=1) as psum_setup:
+            ln_bank = psum_setup.tile([P, P], BF16, name="ln_bank")
+            ln_columns = rows_to_columns("ln_columns", ln_rows, 2 * PACK, ln_bank[:])
+
+            w_grouped = keep.tile([P, P, PACK], BF16, name="w_grouped", align_bytes=64)
+            nc.vector.tensor_copy(out=w_grouped[:], in_=w_planes[:].rearrange("p t c -> p c t"))
+            w_codes = keep.tile([P, P], U32, name="w_codes", align_bytes=64)
+            w_scales = keep.tile([P, P], U8, name="w_scales", align_bytes=64)
+            nc.vector.quantize_mx(
+                out=w_codes[:].bitcast(FP8X4), scales=w_scales[:], in_=w_grouped[:].rearrange("p c t -> p (c t)"))
+
+            quantise(0)
+
+            pair_bank = psum_setup.tile([P, P], BF16, name="pair_bank")
+            pair_columns = rows_to_columns("pair_columns", pair_rows, N_PAIR_COLS, pair_bank[:])
+            nc.vector.reduce_sum(out=bias_total[:], in_=pair_columns[:, COL_BIAS:N_PAIR_COLS], axis=mybir.AxisListType.X)
+
+            def spread(dst, column):
+                nc.tensor.transpose(dst, pair_columns[:, column : column + 1].to_broadcast([P, P]), ident_f[:])
+
+            for m in range(4):
+                spread(spread_a[:, m, :], m)
+            spread(spread_b[:, 0, :], 4)
+            spread(spread_b[:, 1, :], COL_PBM)
+            spread(spread_b[:, 2, :], COL_BBM)
+            w_spread = [spread_a[:, m, :] for m in range(4)] + [spread_b[:, 0, :]]
+
+            nc.vector.scalar_tensor_tensor(
+                out=feat[:, 0, :], in0=small["mc"][:], scalar=pair_columns[:, COL_PBM : COL_PBM + 1], in1=spread_b[:, 1, :],
+                op0=ALU.mult, op1=ALU.mult)
+            nc.vector.scalar_tensor_tensor(
+                out=feat[:, 4, :], in0=small["mc"][:], scalar=pair_columns[:, COL_BBM : COL_BBM + 1], in1=spread_b[:, 2, :],
+                op0=ALU.mult, op1=ALU.mult)
+            for m, name in ((1, "ux"), (2, "uy"), (3, "uz")):
+                nc.vector.tensor_tensor(out=feat[:, m, :], in0=small[name][:], in1=feat[:, 4, :], op=ALU.mult)
+
+            row_term = keep.tile([P, P], F32, name="row_term")
+            nc.vector.tensor_tensor(out=row_term[:], in0=small["aa1"][:], in1=small["esm1"][:], op=ALU.add)
+            col_term = keep.tile([P, P], F32, name="col_term")
+            nc.vector.tensor_tensor(out=col_term[:], in0=small["aa2"][:], in1=small["esm2"][:], op=ALU.add)
+            term_bank = psum_setup.tile([P, 2, P], F32, name="term_bank")
+            nc.tensor.transpose(term_bank[:, 0, :], row_term[:], ident_f[:])
+            nc.tensor.transpose(term_bank[:, 1, :], col_term[:], ident_f[:])
+            nc.vector.tensor_copy(out=row_term_t[:], in_=term_bank[:, 0, :])
+            nc.vector.tensor_scalar(
+                out=col_term_t[:], in0=term_bank[:, 1, :], scalar1=bias_total[:, 0:1], scalar2=None, op0=ALU.add)
+
+        psum_mx = stack.enter_context(tc.psum_pool(name="psum_mx", bufs=1))
+        psum_base = stack.enter_context(tc.psum_pool(name="psum_base", bufs=2))
+
+        for g in range(N_GROUPS):
+            if g + LOAD_AHEAD < N_GROUPS:
+                load(g + LOAD_AHEAD)
+            if g + 2 < N_GROUPS:
+                normalise(g + 2)
+            if g + 1 < N_GROUPS:
+                quantise(g + 1)
+            finish(g)

@@ -16,9 +16,25 @@ C_IN = 512
 PACK = 4
 LN_EPS = 1e-5
 GROUP = 4
+PAIRS = GROUP * P
 N_GROUPS = P // GROUP
 N_FEAT = 5
-LOAD_AHEAD = 3
+X_AHEAD = 4
+VECTOR_PAIRS = PAIRS // 2
+
+ROW_GAIN = 0
+ROW_SHIFT = 4
+ROW_W = 8
+ROW_PBM = 13
+ROW_BBM = 14
+ROW_BIAS = 15
+N_ROWS = 21
+
+LAG_DEVIATIONS = 1
+LAG_NORMALISE = 2
+LAG_TRANSPOSE = 3
+LAG_PROJECT = 4
+N_STEPS = N_GROUPS + LAG_PROJECT
 
 FLOPS = 2 * P * P * C_IN * P
 
@@ -36,93 +52,98 @@ def tile_templatepairembeddermultimer_pa_kernel(
 ):
     nc = tc.nc
     with ExitStack() as stack:
+        stack.enter_context(tc.manual_schedule())
         keep = stack.enter_context(tc.tile_pool(name="keep", bufs=1))
-        x_pool = stack.enter_context(tc.tile_pool(name="x", bufs=LOAD_AHEAD + 3))
-        act_pool = stack.enter_context(tc.tile_pool(name="act", bufs=LOAD_AHEAD + 4))
-        stat_pool = stack.enter_context(tc.tile_pool(name="stat", bufs=6))
-        work = stack.enter_context(tc.tile_pool(name="work", bufs=4))
+        x_pool = stack.enter_context(tc.tile_pool(name="x", bufs=X_AHEAD + LAG_NORMALISE + 1))
+        act_pool = stack.enter_context(tc.tile_pool(name="act", bufs=LAG_PROJECT + 2))
+        stat_pool = stack.enter_context(tc.tile_pool(name="stat", bufs=4))
+        work = stack.enter_context(tc.tile_pool(name="work", bufs=3))
         scrap = stack.enter_context(tc.tile_pool(name="scrap", bufs=4))
         psum_keep = stack.enter_context(tc.psum_pool(name="psum_keep", bufs=1))
-        psum_y = stack.enter_context(tc.psum_pool(name="psum_y", bufs=3))
+        psum_y = stack.enter_context(tc.psum_pool(name="psum_y", bufs=PACK))
 
-        x_tiles = {}
-        act_tiles = {}
-        y_tiles = {}
-        code_tiles = {}
+        x_tiles, act_tiles, neg_means, stds, rstds, y_tiles, y_banks, plane_tiles, code_tiles, res_tiles = (
+            {}, {}, {}, {}, {}, {}, {}, {}, {}, {})
 
-        def load(g):
-            columns = slice(g * GROUP, (g + 1) * GROUP)
+        def columns_of(g):
+            return slice(g * GROUP, (g + 1) * GROUP)
+
+        def load_x(g):
             x_tiles[g] = x_pool.tile([P, GROUP, C_IN], BF16, name="x_g")
-            nc.sync.dma_start(out=x_tiles[g][:], in_=query_embedding[:, columns, :])
+            nc.sync.dma_start(out=x_tiles[g][:], in_=query_embedding[:, columns_of(g), :])
+
+        def load_act(g):
             act_tiles[g] = act_pool.tile([P, GROUP, P], BF16, name="act_g")
-            nc.sync.dma_start(out=act_tiles[g][:], in_=act_dgram[:, columns, :])
+            nc.sync.dma_start(out=act_tiles[g][:], in_=act_dgram[:, columns_of(g), :])
 
-        def load_rows(name, vectors):
-            rows = keep.tile([P, P], BF16, name=name)
-            nc.vector.memset(rows[:], 0.0)
-            first = 0
-            for vector in vectors:
-                n = vector.shape[0]
-                nc.sync.dma_start(out=rows[first : first + n, :], in_=vector)
-                first += n
-            return rows
-
-        def rows_to_columns(name, rows, n_rows, bank):
-            nc.tensor.transpose(bank, rows[:], ident_b[:])
-            columns = keep.tile([P, n_rows], F32, name=name)
-            nc.vector.tensor_copy(out=columns[:], in_=bank[:, 0:n_rows])
-            return columns
-
-        def normalise(g):
-            x_g = x_tiles[g]
+        def row_sums(g):
             row_sum = stat_pool.tile([P, GROUP], F32, name="row_sum")
             for jj in range(GROUP):
                 unread_v = scrap.tile([P, C_IN], BF16, name="unread_v")
                 nc.vector.tensor_scalar(
-                    out=unread_v[:], in0=x_g[:, jj, :], scalar1=1.0, scalar2=None, op0=ALU.mult, op1=ALU.add,
+                    out=unread_v[:], in0=x_tiles[g][:, jj, :], scalar1=1.0, scalar2=None, op0=ALU.mult, op1=ALU.add,
                     accum_out=row_sum[:, jj : jj + 1])
-            neg_mean = stat_pool.tile([P, GROUP], F32, name="neg_mean")
-            nc.vector.tensor_scalar(out=neg_mean[:], in0=row_sum[:], scalar1=-1.0 / C_IN, scalar2=None, op0=ALU.mult)
+            neg_means[g] = stat_pool.tile([P, GROUP], F32, name="neg_mean")
+            nc.vector.tensor_scalar(
+                out=neg_means[g][:], in0=row_sum[:], scalar1=-1.0 / C_IN, scalar2=None, op0=ALU.mult)
+
+        def deviations(g):
             dev_sq = stat_pool.tile([P, GROUP], F32, name="dev_sq")
             for jj in range(GROUP):
                 unread_s = scrap.tile([P, C_IN], BF16, name="unread_s")
                 nc.scalar.activation(
-                    out=unread_s[:], in_=x_g[:, jj, :], func=ACT.Square, bias=neg_mean[:, jj : jj + 1], scale=1.0,
-                    accum_out=dev_sq[:, jj : jj + 1])
-            std = stat_pool.tile([P, GROUP], F32, name="std")
-            nc.scalar.activation(out=std[:], in_=dev_sq[:], func=ACT.Sqrt, bias=eps[:, 0:1], scale=1.0 / C_IN)
-            rstd = stat_pool.tile([P, GROUP], F32, name="rstd")
-            nc.vector.reciprocal(out=rstd[:], in_=std[:])
+                    out=unread_s[:], in_=x_tiles[g][:, jj, :], func=ACT.Square, bias=neg_means[g][:, jj : jj + 1],
+                    scale=1.0, accum_out=dev_sq[:, jj : jj + 1])
+            stds[g] = stat_pool.tile([P, GROUP], F32, name="std")
+            nc.scalar.activation(out=stds[g][:], in_=dev_sq[:], func=ACT.Sqrt, bias=eps[:, 0:1], scale=1.0 / C_IN)
+
+        def inverse_std(g):
+            rstds[g] = stat_pool.tile([P, GROUP], F32, name="rstd")
+            nc.vector.reciprocal(out=rstds[g][:], in_=stds[g][:])
+
+        def normalise(g):
             y_tiles[g] = work.tile([P, GROUP, C_IN], F32, name="y_g")
             for jj in range(GROUP):
                 nc.gpsimd.tensor_scalar(
-                    out=y_tiles[g][:, jj, :], in0=x_g[:, jj, :],
-                    scalar1=neg_mean[:, jj : jj + 1], scalar2=rstd[:, jj : jj + 1], op0=ALU.add, op1=ALU.mult)
+                    out=y_tiles[g][:, jj, :], in0=x_tiles[g][:, jj, :],
+                    scalar1=neg_means[g][:, jj : jj + 1], scalar2=rstds[g][:, jj : jj + 1], op0=ALU.add, op1=ALU.mult)
 
-        def quantise(g):
-            y_g = y_tiles[g]
-            q_planes = work.tile([P, PACK, GROUP * P], BF16, name="q_planes")
+        def transpose(g):
+            y_banks[g] = []
             for t in range(PACK):
                 y_t = psum_y.tile([P, GROUP, P], F32, name="y_t")
                 for jj in range(GROUP):
-                    nc.tensor.transpose(y_t[:, jj, :], y_g[:, jj, t * P : (t + 1) * P], ident_f[:])
+                    nc.tensor.transpose(y_t[:, jj, :], y_tiles[g][:, jj, t * P : (t + 1) * P], ident_f[:])
+                y_banks[g].append(y_t)
+
+        def gain_shift(g):
+            plane_tiles[g] = work.tile([P, PACK, PAIRS], BF16, name="q_planes")
+            for t in range(PACK):
                 nc.scalar.activation(
-                    out=q_planes[:, t, :], in_=y_t[:].rearrange("p a b -> p (a b)"), func=ACT.Identity,
-                    scale=ln_columns[:, t : t + 1], bias=ln_columns[:, PACK + t : PACK + t + 1])
-            q_grouped = work.tile([P, GROUP * P, PACK], BF16, name="q_grouped", align_bytes=64)
-            nc.gpsimd.tensor_scalar(
-                out=q_grouped[:], in0=q_planes[:].rearrange("p t r -> p r t"), scalar1=1.0, scalar2=0.0,
-                op0=ALU.mult, op1=ALU.add)
-            q_codes = work.tile([P, GROUP * P], U32, name="q_codes", align_bytes=64)
-            q_scales = work.tile([P, GROUP * P], U8, name="q_scales", align_bytes=64)
+                    out=plane_tiles[g][:, t, :], in_=y_banks[g][t][:].rearrange("p a b -> p (a b)"), func=ACT.Identity,
+                    scale=columns[:, ROW_GAIN + t : ROW_GAIN + t + 1], bias=columns[:, ROW_SHIFT + t : ROW_SHIFT + t + 1])
+
+        def regroup(g):
+            q_planes = plane_tiles[g]
+            q_grouped = work.tile([P, PAIRS, PACK], BF16, name="q_grouped", align_bytes=64)
+            nc.vector.tensor_copy(
+                out=q_grouped[:, 0:VECTOR_PAIRS, :].rearrange("p (c i) t -> p c t i", i=4),
+                in_=q_planes[:, :, 0:VECTOR_PAIRS].rearrange("p t (c i) -> p c t i", i=4))
+            nc.scalar.copy(
+                out=q_grouped[:, VECTOR_PAIRS:, :].rearrange("p (c i) t -> p c t i", i=4),
+                in_=q_planes[:, :, VECTOR_PAIRS:].rearrange("p t (c i) -> p c t i", i=4))
+            return q_grouped
+
+        def quantise(g, q_grouped):
+            q_codes = work.tile([P, PAIRS], U32, name="q_codes", align_bytes=64)
+            q_scales = work.tile([P, PAIRS], U8, name="q_scales", align_bytes=64)
             nc.vector.quantize_mx(
                 out=q_codes[:].bitcast(FP8X4), scales=q_scales[:], in_=q_grouped[:].rearrange("p r t -> p (r t)"))
             code_tiles[g] = (q_codes, q_scales)
 
-        def finish(g):
+        def project(g):
             q_codes, q_scales = code_tiles[g]
-            act_g = act_tiles[g]
-            proj_ps = psum_mx.tile([P, GROUP * P], F32, name="proj_ps")
+            proj_ps = psum_mx.tile([P, PAIRS], F32, name="proj_ps")
             nc.tensor.matmul_mx(
                 out=proj_ps[:],
                 lhsT=w_codes[:].bitcast(FP8X4), lhsT_scale=w_scales[:],
@@ -130,6 +151,9 @@ def tile_templatepairembeddermultimer_pa_kernel(
                 start=True, stop=True)
             proj_t = work.tile([P, GROUP, P], F32, name="proj_t")
             nc.scalar.copy(out=proj_t[:].rearrange("p a b -> p (a b)"), in_=proj_ps[:])
+            return proj_t
+
+        def turn_back(g, proj_t):
             base = psum_base.tile([P, GROUP, P], F32, name="base")
             for jj in range(GROUP):
                 j = g * GROUP + jj
@@ -139,19 +163,53 @@ def tile_templatepairembeddermultimer_pa_kernel(
                                  is_transpose=True, start=False, stop=False)
                 nc.tensor.matmul(out=base[:, jj, :], lhsT=proj_t[:, jj, :], rhs=ident_f[:], is_transpose=True,
                                  start=False, stop=True)
-            res = work.tile([P, GROUP, P], F32, name="res")
+            return base
+
+        def rank_one(g):
+            res_tiles[g] = work.tile([P, GROUP, P], F32, name="res")
             for m in range(N_FEAT):
                 for jj in range(GROUP):
                     j = g * GROUP + jj
                     nc.vector.scalar_tensor_tensor(
-                        out=res[:, jj, :], in0=w_spread[m], scalar=feat[:, m, j : j + 1],
-                        in1=act_g[:, jj, :] if m == 0 else res[:, jj, :], op0=ALU.mult, op1=ALU.add)
-            nc.vector.tensor_tensor(out=res[:], in0=res[:], in1=base[:], op=ALU.add)
-            nc.sync.dma_start(out=out[:, g * GROUP : (g + 1) * GROUP, :], in_=res[:])
+                        out=res_tiles[g][:, jj, :], in0=w_spread[m], scalar=feat[:, m, j : j + 1],
+                        in1=act_tiles[g][:, jj, :] if m == 0 else res_tiles[g][:, jj, :], op0=ALU.mult, op1=ALU.add)
 
-        load(0)
+        def add_store(g, base):
+            nc.vector.tensor_tensor(out=res_tiles[g][:], in0=res_tiles[g][:], in1=base[:], op=ALU.add)
+            nc.sync.dma_start(out=out[:, columns_of(g), :], in_=res_tiles[g][:])
+
+        def step(s):
+            if s + X_AHEAD < N_GROUPS:
+                load_x(s + X_AHEAD)
+            if s < N_GROUPS:
+                load_act(s)
+            first, second, third, last = s, s - LAG_DEVIATIONS, s - LAG_NORMALISE, s - LAG_PROJECT
+            turning = s - LAG_TRANSPOSE
+            if 0 <= third < N_GROUPS:
+                inverse_std(third)
+                normalise(third)
+            if 0 <= turning < N_GROUPS:
+                transpose(turning)
+            if 0 <= last:
+                q_grouped = regroup(last)
+            if first < N_GROUPS:
+                row_sums(first)
+            if 0 <= second < N_GROUPS:
+                deviations(second)
+            if 0 <= last:
+                quantise(last, q_grouped)
+                proj_t = project(last)
+            if 0 <= turning < N_GROUPS:
+                gain_shift(turning)
+            if 0 <= last:
+                base = turn_back(last, proj_t)
+                rank_one(last)
+                add_store(last, base)
+
         eps = keep.tile([P, 1], F32, name="eps")
         nc.vector.memset(eps[:], LN_EPS)
+        rows = keep.tile([P, P], BF16, name="rows")
+        nc.vector.memset(rows[:], 0.0)
         table_warm = keep.tile([P, 1], F32, name="table_warm")
         nc.scalar.activation(out=table_warm[:], in_=eps[:], func=ACT.Sqrt)
         ident_f = keep.tile([P, P], F32, name="ident_f")
@@ -159,14 +217,18 @@ def tile_templatepairembeddermultimer_pa_kernel(
         ident_b = keep.tile([P, P], BF16, name="ident_b")
         make_identity(nc, ident_b[:])
 
-        ln_rows = load_rows("ln_rows", (ln_g.rearrange("(t p) -> t p", p=P), ln_b.rearrange("(t p) -> t p", p=P)))
+        load_x(0)
+        load_x(1)
+        nc.sync.dma_start(out=rows[ROW_GAIN : ROW_GAIN + PACK, :], in_=ln_g.rearrange("(t p) -> t p", p=P))
+        nc.sync.dma_start(out=rows[ROW_SHIFT : ROW_SHIFT + PACK, :], in_=ln_b.rearrange("(t p) -> t p", p=P))
+        for n, row in enumerate((w_pbm, w_x, w_y, w_z, w_bb, as_row(pseudo_beta_mask), as_row(backbone_mask))):
+            nc.sync.dma_start(out=rows[ROW_W + n : ROW_W + n + 1, :], in_=row)
+        load_x(2)
+        for n, vector in enumerate((b_q, b_pbm, b_x, b_y, b_z, b_bb)):
+            nc.sync.dma_start(out=rows[ROW_BIAS + n : ROW_BIAS + n + 1, :], in_=as_row(vector))
         w_planes = keep.tile([P, PACK, P], BF16, name="w_planes")
         nc.sync.dma_start(out=w_planes[:], in_=w_q.rearrange("(t p) c -> p t c", p=P))
-        load(1)
-        pair_rows = load_rows(
-            "pair_rows", (w_pbm, w_x, w_y, w_z, w_bb, as_row(pseudo_beta_mask), as_row(backbone_mask),
-                          as_row(b_q), as_row(b_pbm), as_row(b_x), as_row(b_y), as_row(b_z), as_row(b_bb)))
-        COL_PBM, COL_BBM, COL_BIAS, N_PAIR_COLS = 5, 6, 7, 13
+        load_x(3)
         small = {}
         for name, matrix in (
             ("mc", multichain_mask_2d), ("ux", unit_x), ("uy", unit_y), ("uz", unit_z),
@@ -174,11 +236,11 @@ def tile_templatepairembeddermultimer_pa_kernel(
         ):
             small[name] = keep.tile([P, P], BF16, name="in_" + name)
             nc.sync.dma_start(out=small[name][:], in_=matrix)
-        load(2)
 
-        normalise(0)
-        normalise(1)
+        for s in range(LAG_TRANSPOSE):
+            step(s)
 
+        columns = keep.tile([P, N_ROWS], F32, name="columns")
         bias_total = keep.tile([P, 1], F32, name="bias_total")
         row_term_t = keep.tile([P, P], F32, name="row_term_t")
         col_term_t = keep.tile([P, P], F32, name="col_term_t")
@@ -186,9 +248,20 @@ def tile_templatepairembeddermultimer_pa_kernel(
         spread_a = psum_keep.tile([P, 4, P], F32, name="spread_a")
         spread_b = psum_keep.tile([P, 3, P], F32, name="spread_b")
 
+        def spread(dst, row):
+            nc.tensor.transpose(dst, columns[:, row : row + 1].to_broadcast([P, P]), ident_f[:])
+
         with tc.psum_pool(name="psum_setup", bufs=1) as psum_setup:
-            ln_bank = psum_setup.tile([P, P], BF16, name="ln_bank")
-            ln_columns = rows_to_columns("ln_columns", ln_rows, 2 * PACK, ln_bank[:])
+            rows_t = psum_setup.tile([P, P], BF16, name="rows_t")
+            nc.tensor.transpose(rows_t[:], rows[:], ident_b[:])
+            nc.vector.tensor_copy(out=columns[:], in_=rows_t[:, 0:N_ROWS])
+            for m in range(4):
+                spread(spread_a[:, m, :], ROW_W + m)
+            spread(spread_b[:, 0, :], ROW_W + 4)
+            spread(spread_b[:, 1, :], ROW_PBM)
+            spread(spread_b[:, 2, :], ROW_BBM)
+            w_spread = [spread_a[:, m, :] for m in range(4)] + [spread_b[:, 0, :]]
+            nc.vector.reduce_sum(out=bias_total[:], in_=columns[:, ROW_BIAS:N_ROWS], axis=mybir.AxisListType.X)
 
             w_grouped = keep.tile([P, P, PACK], BF16, name="w_grouped", align_bytes=64)
             nc.vector.tensor_copy(out=w_grouped[:], in_=w_planes[:].rearrange("p t c -> p c t"))
@@ -197,27 +270,11 @@ def tile_templatepairembeddermultimer_pa_kernel(
             nc.vector.quantize_mx(
                 out=w_codes[:].bitcast(FP8X4), scales=w_scales[:], in_=w_grouped[:].rearrange("p c t -> p (c t)"))
 
-            quantise(0)
-
-            pair_bank = psum_setup.tile([P, P], BF16, name="pair_bank")
-            pair_columns = rows_to_columns("pair_columns", pair_rows, N_PAIR_COLS, pair_bank[:])
-            nc.vector.reduce_sum(out=bias_total[:], in_=pair_columns[:, COL_BIAS:N_PAIR_COLS], axis=mybir.AxisListType.X)
-
-            def spread(dst, column):
-                nc.tensor.transpose(dst, pair_columns[:, column : column + 1].to_broadcast([P, P]), ident_f[:])
-
-            for m in range(4):
-                spread(spread_a[:, m, :], m)
-            spread(spread_b[:, 0, :], 4)
-            spread(spread_b[:, 1, :], COL_PBM)
-            spread(spread_b[:, 2, :], COL_BBM)
-            w_spread = [spread_a[:, m, :] for m in range(4)] + [spread_b[:, 0, :]]
-
             nc.vector.scalar_tensor_tensor(
-                out=feat[:, 0, :], in0=small["mc"][:], scalar=pair_columns[:, COL_PBM : COL_PBM + 1], in1=spread_b[:, 1, :],
+                out=feat[:, 0, :], in0=small["mc"][:], scalar=columns[:, ROW_PBM : ROW_PBM + 1], in1=spread_b[:, 1, :],
                 op0=ALU.mult, op1=ALU.mult)
             nc.vector.scalar_tensor_tensor(
-                out=feat[:, 4, :], in0=small["mc"][:], scalar=pair_columns[:, COL_BBM : COL_BBM + 1], in1=spread_b[:, 2, :],
+                out=feat[:, 4, :], in0=small["mc"][:], scalar=columns[:, ROW_BBM : ROW_BBM + 1], in1=spread_b[:, 2, :],
                 op0=ALU.mult, op1=ALU.mult)
             for m, name in ((1, "ux"), (2, "uy"), (3, "uz")):
                 nc.vector.tensor_tensor(out=feat[:, m, :], in0=small[name][:], in1=feat[:, 4, :], op=ALU.mult)
@@ -234,13 +291,7 @@ def tile_templatepairembeddermultimer_pa_kernel(
                 out=col_term_t[:], in0=term_bank[:, 1, :], scalar1=bias_total[:, 0:1], scalar2=None, op0=ALU.add)
 
         psum_mx = stack.enter_context(tc.psum_pool(name="psum_mx", bufs=1))
-        psum_base = stack.enter_context(tc.psum_pool(name="psum_base", bufs=2))
+        psum_base = stack.enter_context(tc.psum_pool(name="psum_base", bufs=1))
 
-        for g in range(N_GROUPS):
-            if g + LOAD_AHEAD < N_GROUPS:
-                load(g + LOAD_AHEAD)
-            if g + 2 < N_GROUPS:
-                normalise(g + 2)
-            if g + 1 < N_GROUPS:
-                quantise(g + 1)
-            finish(g)
+        for s in range(LAG_TRANSPOSE, N_STEPS):
+            step(s)

@@ -20,7 +20,8 @@ PAIRS = GROUP * P
 N_GROUPS = P // GROUP
 N_FEAT = 5
 X_AHEAD = 4
-VECTOR_PAIRS = PAIRS // 2
+VECTOR_COLUMNS = 2
+GPSIMD_PAIRS = 3 * PAIRS // 4
 
 ROW_GAIN = 0
 ROW_SHIFT = 4
@@ -30,11 +31,11 @@ ROW_BBM = 14
 ROW_BIAS = 15
 N_ROWS = 21
 
-LAG_DEVIATIONS = 1
 LAG_NORMALISE = 2
 LAG_TRANSPOSE = 3
 LAG_PROJECT = 4
-N_STEPS = N_GROUPS + LAG_PROJECT
+LAG_STORE = 5
+N_STEPS = N_GROUPS + LAG_STORE
 
 FLOPS = 2 * P * P * C_IN * P
 
@@ -62,8 +63,8 @@ def tile_templatepairembeddermultimer_pa_kernel(
         psum_keep = stack.enter_context(tc.psum_pool(name="psum_keep", bufs=1))
         psum_y = stack.enter_context(tc.psum_pool(name="psum_y", bufs=PACK))
 
-        x_tiles, act_tiles, neg_means, stds, rstds, y_tiles, y_banks, plane_tiles, code_tiles, res_tiles = (
-            {}, {}, {}, {}, {}, {}, {}, {}, {}, {})
+        x_tiles, act_tiles, vector_stats, neg_means, stds, rstds, y_tiles, y_banks, plane_tiles, res_tiles, bases = (
+            {}, {}, {}, {}, {}, {}, {}, {}, {}, {}, {})
 
         def columns_of(g):
             return slice(g * GROUP, (g + 1) * GROUP)
@@ -76,26 +77,38 @@ def tile_templatepairembeddermultimer_pa_kernel(
             act_tiles[g] = act_pool.tile([P, GROUP, P], BF16, name="act_g")
             nc.sync.dma_start(out=act_tiles[g][:], in_=act_dgram[:, columns_of(g), :])
 
-        def row_sums(g):
-            row_sum = stat_pool.tile([P, GROUP], F32, name="row_sum")
-            for jj in range(GROUP):
-                unread_v = scrap.tile([P, C_IN], BF16, name="unread_v")
-                nc.vector.tensor_scalar(
-                    out=unread_v[:], in0=x_tiles[g][:, jj, :], scalar1=1.0, scalar2=None, op0=ALU.mult, op1=ALU.add,
-                    accum_out=row_sum[:, jj : jj + 1])
-            neg_means[g] = stat_pool.tile([P, GROUP], F32, name="neg_mean")
-            nc.vector.tensor_scalar(
-                out=neg_means[g][:], in0=row_sum[:], scalar1=-1.0 / C_IN, scalar2=None, op0=ALU.mult)
+        def vector_statistics(g):
+            vector_stats[g] = stat_pool.tile([P, VECTOR_COLUMNS, 2], F32, name="mean_var")
+            for jj in range(VECTOR_COLUMNS):
+                partial = stat_pool.tile([P, 6], F32, name="partial")
+                nc.vector.bn_stats(out=partial[:], in_=x_tiles[g][:, jj, :])
+                nc.vector.bn_aggr(out=vector_stats[g][:, jj, :], in_=partial[:])
 
-        def deviations(g):
-            dev_sq = stat_pool.tile([P, GROUP], F32, name="dev_sq")
-            for jj in range(GROUP):
-                unread_s = scrap.tile([P, C_IN], BF16, name="unread_s")
-                nc.scalar.activation(
-                    out=unread_s[:], in_=x_tiles[g][:, jj, :], func=ACT.Square, bias=neg_means[g][:, jj : jj + 1],
-                    scale=1.0, accum_out=dev_sq[:, jj : jj + 1])
+        def scalar_statistics(g):
+            neg_means[g] = stat_pool.tile([P, GROUP], F32, name="neg_mean")
             stds[g] = stat_pool.tile([P, GROUP], F32, name="std")
-            nc.scalar.activation(out=stds[g][:], in_=dev_sq[:], func=ACT.Sqrt, bias=eps[:, 0:1], scale=1.0 / C_IN)
+            row_sum = stat_pool.tile([P, GROUP - VECTOR_COLUMNS], F32, name="row_sum")
+            dev_sq = stat_pool.tile([P, GROUP - VECTOR_COLUMNS], F32, name="dev_sq")
+            for jj in range(VECTOR_COLUMNS, GROUP):
+                unread = scrap.tile([P, C_IN], BF16, name="unread")
+                nc.scalar.activation(
+                    out=unread[:], in_=x_tiles[g][:, jj, :], func=ACT.Identity,
+                    accum_out=row_sum[:, jj - VECTOR_COLUMNS : jj - VECTOR_COLUMNS + 1])
+            nc.scalar.mul(out=neg_means[g][:, VECTOR_COLUMNS:], in_=row_sum[:], mul=-1.0 / C_IN)
+            if g > 0:
+                finish_vector_statistics(g - 1)
+            for jj in range(VECTOR_COLUMNS, GROUP):
+                unread = scrap.tile([P, C_IN], BF16, name="unread")
+                nc.scalar.activation(
+                    out=unread[:], in_=x_tiles[g][:, jj, :], func=ACT.Square, bias=neg_means[g][:, jj : jj + 1],
+                    scale=1.0, accum_out=dev_sq[:, jj - VECTOR_COLUMNS : jj - VECTOR_COLUMNS + 1])
+            nc.scalar.activation(
+                out=stds[g][:, VECTOR_COLUMNS:], in_=dev_sq[:], func=ACT.Sqrt, bias=eps[:, 0:1], scale=1.0 / C_IN)
+
+        def finish_vector_statistics(g):
+            nc.scalar.mul(out=neg_means[g][:, 0:VECTOR_COLUMNS], in_=vector_stats[g][:, :, 0], mul=-1.0)
+            nc.scalar.activation(
+                out=stds[g][:, 0:VECTOR_COLUMNS], in_=vector_stats[g][:, :, 1], func=ACT.Sqrt, bias=eps[:, 0:1], scale=1.0)
 
         def inverse_std(g):
             rstds[g] = stat_pool.tile([P, GROUP], F32, name="rstd")
@@ -126,12 +139,12 @@ def tile_templatepairembeddermultimer_pa_kernel(
         def regroup(g):
             q_planes = plane_tiles[g]
             q_grouped = work.tile([P, PAIRS, PACK], BF16, name="q_grouped", align_bytes=64)
-            nc.vector.tensor_copy(
-                out=q_grouped[:, 0:VECTOR_PAIRS, :].rearrange("p (c i) t -> p c t i", i=4),
-                in_=q_planes[:, :, 0:VECTOR_PAIRS].rearrange("p t (c i) -> p c t i", i=4))
+            nc.gpsimd.tensor_scalar(
+                out=q_grouped[:, 0:GPSIMD_PAIRS, :], in0=q_planes[:, :, 0:GPSIMD_PAIRS].rearrange("p t r -> p r t"),
+                scalar1=1.0, scalar2=0.0, op0=ALU.mult, op1=ALU.add)
             nc.scalar.copy(
-                out=q_grouped[:, VECTOR_PAIRS:, :].rearrange("p (c i) t -> p c t i", i=4),
-                in_=q_planes[:, :, VECTOR_PAIRS:].rearrange("p t (c i) -> p c t i", i=4))
+                out=q_grouped[:, GPSIMD_PAIRS:, :].rearrange("p (c i) t -> p c t i", i=4),
+                in_=q_planes[:, :, GPSIMD_PAIRS:].rearrange("p t (c i) -> p c t i", i=4))
             return q_grouped
 
         def quantise(g, q_grouped):
@@ -139,10 +152,9 @@ def tile_templatepairembeddermultimer_pa_kernel(
             q_scales = work.tile([P, PAIRS], U8, name="q_scales", align_bytes=64)
             nc.vector.quantize_mx(
                 out=q_codes[:].bitcast(FP8X4), scales=q_scales[:], in_=q_grouped[:].rearrange("p r t -> p (r t)"))
-            code_tiles[g] = (q_codes, q_scales)
+            return q_codes, q_scales
 
-        def project(g):
-            q_codes, q_scales = code_tiles[g]
+        def project(q_codes, q_scales):
             proj_ps = psum_mx.tile([P, PAIRS], F32, name="proj_ps")
             nc.tensor.matmul_mx(
                 out=proj_ps[:],
@@ -155,6 +167,7 @@ def tile_templatepairembeddermultimer_pa_kernel(
 
         def turn_back(g, proj_t):
             base = psum_base.tile([P, GROUP, P], F32, name="base")
+            bases[g] = base
             for jj in range(GROUP):
                 j = g * GROUP + jj
                 nc.tensor.matmul(out=base[:, jj, :], lhsT=col_term_t[:], rhs=ident_f[:], is_transpose=True,
@@ -163,7 +176,6 @@ def tile_templatepairembeddermultimer_pa_kernel(
                                  is_transpose=True, start=False, stop=False)
                 nc.tensor.matmul(out=base[:, jj, :], lhsT=proj_t[:, jj, :], rhs=ident_f[:], is_transpose=True,
                                  start=False, stop=True)
-            return base
 
         def rank_one(g):
             res_tiles[g] = work.tile([P, GROUP, P], F32, name="res")
@@ -174,37 +186,39 @@ def tile_templatepairembeddermultimer_pa_kernel(
                         out=res_tiles[g][:, jj, :], in0=w_spread[m], scalar=feat[:, m, j : j + 1],
                         in1=act_tiles[g][:, jj, :] if m == 0 else res_tiles[g][:, jj, :], op0=ALU.mult, op1=ALU.add)
 
-        def add_store(g, base):
-            nc.vector.tensor_tensor(out=res_tiles[g][:], in0=res_tiles[g][:], in1=base[:], op=ALU.add)
+        def add_store(g):
+            nc.vector.tensor_tensor(out=res_tiles[g][:], in0=res_tiles[g][:], in1=bases[g][:], op=ALU.add)
             nc.sync.dma_start(out=out[:, columns_of(g), :], in_=res_tiles[g][:])
 
         def step(s):
+            entering, normalising, turning, projecting, leaving = (
+                s, s - LAG_NORMALISE, s - LAG_TRANSPOSE, s - LAG_PROJECT, s - LAG_STORE)
             if s + X_AHEAD < N_GROUPS:
                 load_x(s + X_AHEAD)
-            if s < N_GROUPS:
-                load_act(s)
-            first, second, third, last = s, s - LAG_DEVIATIONS, s - LAG_NORMALISE, s - LAG_PROJECT
-            turning = s - LAG_TRANSPOSE
-            if 0 <= third < N_GROUPS:
-                inverse_std(third)
-                normalise(third)
+            if entering < N_GROUPS:
+                load_act(entering)
+            if 0 <= leaving:
+                add_store(leaving)
+            if 0 <= projecting < N_GROUPS:
+                q_grouped = regroup(projecting)
+            if 0 <= normalising < N_GROUPS:
+                inverse_std(normalising)
+                normalise(normalising)
             if 0 <= turning < N_GROUPS:
                 transpose(turning)
-            if 0 <= last:
-                q_grouped = regroup(last)
-            if first < N_GROUPS:
-                row_sums(first)
-            if 0 <= second < N_GROUPS:
-                deviations(second)
-            if 0 <= last:
-                quantise(last, q_grouped)
-                proj_t = project(last)
+            if entering < N_GROUPS:
+                vector_statistics(entering)
+                scalar_statistics(entering)
+            if entering == N_GROUPS:
+                finish_vector_statistics(N_GROUPS - 1)
+            if 0 <= projecting < N_GROUPS:
+                q_codes, q_scales = quantise(projecting, q_grouped)
+                proj_t = project(q_codes, q_scales)
             if 0 <= turning < N_GROUPS:
                 gain_shift(turning)
-            if 0 <= last:
-                base = turn_back(last, proj_t)
-                rank_one(last)
-                add_store(last, base)
+            if 0 <= projecting < N_GROUPS:
+                turn_back(projecting, proj_t)
+                rank_one(projecting)
 
         eps = keep.tile([P, 1], F32, name="eps")
         nc.vector.memset(eps[:], LN_EPS)

@@ -33,8 +33,10 @@ N_ROWS = 21
 
 LAG_NORMALISE = 2
 LAG_TRANSPOSE = 3
-LAG_PROJECT = 4
-LAG_STORE = 5
+LAG_REGROUP = 4
+LAG_PROJECT = 5
+LAG_TURN_BACK = 6
+LAG_STORE = 7
 N_STEPS = N_GROUPS + LAG_STORE
 
 FLOPS = 2 * P * P * C_IN * P
@@ -56,15 +58,16 @@ def tile_templatepairembeddermultimer_pa_kernel(
         stack.enter_context(tc.manual_schedule())
         keep = stack.enter_context(tc.tile_pool(name="keep", bufs=1))
         x_pool = stack.enter_context(tc.tile_pool(name="x", bufs=X_AHEAD + LAG_NORMALISE + 1))
-        act_pool = stack.enter_context(tc.tile_pool(name="act", bufs=LAG_PROJECT + 2))
+        act_pool = stack.enter_context(tc.tile_pool(name="act", bufs=LAG_TURN_BACK + 2))
         stat_pool = stack.enter_context(tc.tile_pool(name="stat", bufs=4))
         work = stack.enter_context(tc.tile_pool(name="work", bufs=3))
         scrap = stack.enter_context(tc.tile_pool(name="scrap", bufs=4))
         psum_keep = stack.enter_context(tc.psum_pool(name="psum_keep", bufs=1))
         psum_y = stack.enter_context(tc.psum_pool(name="psum_y", bufs=PACK))
 
-        x_tiles, act_tiles, vector_stats, neg_means, stds, rstds, y_tiles, y_banks, plane_tiles, res_tiles, bases = (
-            {}, {}, {}, {}, {}, {}, {}, {}, {}, {}, {})
+        x_tiles, act_tiles, vector_stats, neg_means, stds, rstds, y_tiles, y_banks, plane_tiles = (
+            {}, {}, {}, {}, {}, {}, {}, {}, {})
+        grouped_tiles, code_tiles, proj_banks, proj_tiles, res_tiles, bases = {}, {}, {}, {}, {}, {}
 
         def columns_of(g):
             return slice(g * GROUP, (g + 1) * GROUP)
@@ -139,33 +142,35 @@ def tile_templatepairembeddermultimer_pa_kernel(
         def regroup(g):
             q_planes = plane_tiles[g]
             q_grouped = work.tile([P, PAIRS, PACK], BF16, name="q_grouped", align_bytes=64)
+            grouped_tiles[g] = q_grouped
             nc.gpsimd.tensor_scalar(
                 out=q_grouped[:, 0:GPSIMD_PAIRS, :], in0=q_planes[:, :, 0:GPSIMD_PAIRS].rearrange("p t r -> p r t"),
                 scalar1=1.0, scalar2=0.0, op0=ALU.mult, op1=ALU.add)
             nc.scalar.copy(
                 out=q_grouped[:, GPSIMD_PAIRS:, :].rearrange("p (c i) t -> p c t i", i=4),
                 in_=q_planes[:, :, GPSIMD_PAIRS:].rearrange("p t (c i) -> p c t i", i=4))
-            return q_grouped
 
-        def quantise(g, q_grouped):
+        def quantise(g):
             q_codes = work.tile([P, PAIRS], U32, name="q_codes", align_bytes=64)
             q_scales = work.tile([P, PAIRS], U8, name="q_scales", align_bytes=64)
             nc.vector.quantize_mx(
-                out=q_codes[:].bitcast(FP8X4), scales=q_scales[:], in_=q_grouped[:].rearrange("p r t -> p (r t)"))
-            return q_codes, q_scales
+                out=q_codes[:].bitcast(FP8X4), scales=q_scales[:], in_=grouped_tiles[g][:].rearrange("p r t -> p (r t)"))
+            code_tiles[g] = (q_codes, q_scales)
 
-        def project(q_codes, q_scales):
-            proj_ps = psum_mx.tile([P, PAIRS], F32, name="proj_ps")
+        def project(g):
+            q_codes, q_scales = code_tiles[g]
+            proj_banks[g] = psum_mx.tile([P, PAIRS], F32, name="proj_ps")
             nc.tensor.matmul_mx(
-                out=proj_ps[:],
+                out=proj_banks[g][:],
                 lhsT=w_codes[:].bitcast(FP8X4), lhsT_scale=w_scales[:],
                 rhs=q_codes[:].bitcast(FP8X4), rhs_scale=q_scales[:],
                 start=True, stop=True)
-            proj_t = work.tile([P, GROUP, P], F32, name="proj_t")
-            nc.scalar.copy(out=proj_t[:].rearrange("p a b -> p (a b)"), in_=proj_ps[:])
-            return proj_t
 
-        def turn_back(g, proj_t):
+        def copy_out(g):
+            proj_tiles[g] = work.tile([P, GROUP, P], F32, name="proj_t")
+            nc.scalar.copy(out=proj_tiles[g][:].rearrange("p a b -> p (a b)"), in_=proj_banks[g][:])
+
+        def turn_back(g):
             base = psum_base.tile([P, GROUP, P], F32, name="base")
             bases[g] = base
             for jj in range(GROUP):
@@ -174,7 +179,7 @@ def tile_templatepairembeddermultimer_pa_kernel(
                                  start=True, stop=False)
                 nc.tensor.matmul(out=base[:, jj, :], lhsT=row_term_t[:, j : j + 1].to_broadcast([P, P]), rhs=ident_f[:],
                                  is_transpose=True, start=False, stop=False)
-                nc.tensor.matmul(out=base[:, jj, :], lhsT=proj_t[:, jj, :], rhs=ident_f[:], is_transpose=True,
+                nc.tensor.matmul(out=base[:, jj, :], lhsT=proj_tiles[g][:, jj, :], rhs=ident_f[:], is_transpose=True,
                                  start=False, stop=True)
 
         def rank_one(g):
@@ -190,35 +195,40 @@ def tile_templatepairembeddermultimer_pa_kernel(
             nc.vector.tensor_tensor(out=res_tiles[g][:], in0=res_tiles[g][:], in1=bases[g][:], op=ALU.add)
             nc.sync.dma_start(out=out[:, columns_of(g), :], in_=res_tiles[g][:])
 
+        def in_range(g):
+            return 0 <= g < N_GROUPS
+
         def step(s):
-            entering, normalising, turning, projecting, leaving = (
-                s, s - LAG_NORMALISE, s - LAG_TRANSPOSE, s - LAG_PROJECT, s - LAG_STORE)
-            if s + X_AHEAD < N_GROUPS:
+            if in_range(s + X_AHEAD):
                 load_x(s + X_AHEAD)
-            if entering < N_GROUPS:
-                load_act(entering)
-            if 0 <= leaving:
-                add_store(leaving)
-            if 0 <= projecting < N_GROUPS:
-                q_grouped = regroup(projecting)
-            if 0 <= normalising < N_GROUPS:
-                inverse_std(normalising)
-                normalise(normalising)
-            if 0 <= turning < N_GROUPS:
-                transpose(turning)
-            if entering < N_GROUPS:
-                vector_statistics(entering)
-                scalar_statistics(entering)
-            if entering == N_GROUPS:
+            if in_range(s):
+                load_act(s)
+            if in_range(s - LAG_PROJECT):
+                quantise(s - LAG_PROJECT)
+            if in_range(s - LAG_STORE):
+                add_store(s - LAG_STORE)
+            if in_range(s - LAG_REGROUP):
+                regroup(s - LAG_REGROUP)
+            if in_range(s - LAG_NORMALISE):
+                inverse_std(s - LAG_NORMALISE)
+                normalise(s - LAG_NORMALISE)
+            if in_range(s - LAG_TRANSPOSE):
+                transpose(s - LAG_TRANSPOSE)
+            if in_range(s - LAG_PROJECT):
+                project(s - LAG_PROJECT)
+            if in_range(s - LAG_TURN_BACK):
+                turn_back(s - LAG_TURN_BACK)
+            if in_range(s):
+                vector_statistics(s)
+                scalar_statistics(s)
+            if s == N_GROUPS:
                 finish_vector_statistics(N_GROUPS - 1)
-            if 0 <= projecting < N_GROUPS:
-                q_codes, q_scales = quantise(projecting, q_grouped)
-                proj_t = project(q_codes, q_scales)
-            if 0 <= turning < N_GROUPS:
-                gain_shift(turning)
-            if 0 <= projecting < N_GROUPS:
-                turn_back(projecting, proj_t)
-                rank_one(projecting)
+            if in_range(s - LAG_TRANSPOSE):
+                gain_shift(s - LAG_TRANSPOSE)
+            if in_range(s - LAG_PROJECT):
+                copy_out(s - LAG_PROJECT)
+            if in_range(s - LAG_TURN_BACK):
+                rank_one(s - LAG_TURN_BACK)
 
         eps = keep.tile([P, 1], F32, name="eps")
         nc.vector.memset(eps[:], LN_EPS)

@@ -31,12 +31,13 @@ ROW_BBM = 14
 ROW_BIAS = 15
 N_ROWS = 21
 
-LAG_NORMALISE = 2
-LAG_TRANSPOSE = 3
-LAG_REGROUP = 4
-LAG_PROJECT = 5
-LAG_TURN_BACK = 6
-LAG_STORE = 7
+LAG_NORMALISE = 1
+LAG_TRANSPOSE = 2
+LAG_REGROUP = 3
+LAG_PROJECT = 4
+LAG_TURN_BACK = 5
+LAG_STORE = 6
+LAG_RANK_ONE = 3
 N_STEPS = N_GROUPS + LAG_STORE
 
 FLOPS = 2 * P * P * C_IN * P
@@ -58,10 +59,11 @@ def tile_templatepairembeddermultimer_pa_kernel(
         stack.enter_context(tc.manual_schedule())
         keep = stack.enter_context(tc.tile_pool(name="keep", bufs=1))
         x_pool = stack.enter_context(tc.tile_pool(name="x", bufs=X_AHEAD + LAG_NORMALISE + 1))
-        act_pool = stack.enter_context(tc.tile_pool(name="act", bufs=LAG_TURN_BACK + 2))
+        act_pool = stack.enter_context(tc.tile_pool(name="act", bufs=LAG_RANK_ONE + 2))
         stat_pool = stack.enter_context(tc.tile_pool(name="stat", bufs=4))
         work = stack.enter_context(tc.tile_pool(name="work", bufs=3))
         scrap = stack.enter_context(tc.tile_pool(name="scrap", bufs=4))
+        res_pool = stack.enter_context(tc.tile_pool(name="res", bufs=LAG_STORE - LAG_RANK_ONE + 2))
         psum_keep = stack.enter_context(tc.psum_pool(name="psum_keep", bufs=1))
         psum_y = stack.enter_context(tc.psum_pool(name="psum_y", bufs=PACK))
 
@@ -87,19 +89,19 @@ def tile_templatepairembeddermultimer_pa_kernel(
                 nc.vector.bn_stats(out=partial[:], in_=x_tiles[g][:, jj, :])
                 nc.vector.bn_aggr(out=vector_stats[g][:, jj, :], in_=partial[:])
 
-        def scalar_statistics(g):
+        def scalar_sums(g):
             neg_means[g] = stat_pool.tile([P, GROUP], F32, name="neg_mean")
-            stds[g] = stat_pool.tile([P, GROUP], F32, name="std")
             row_sum = stat_pool.tile([P, GROUP - VECTOR_COLUMNS], F32, name="row_sum")
-            dev_sq = stat_pool.tile([P, GROUP - VECTOR_COLUMNS], F32, name="dev_sq")
             for jj in range(VECTOR_COLUMNS, GROUP):
                 unread = scrap.tile([P, C_IN], BF16, name="unread")
                 nc.scalar.activation(
                     out=unread[:], in_=x_tiles[g][:, jj, :], func=ACT.Identity,
                     accum_out=row_sum[:, jj - VECTOR_COLUMNS : jj - VECTOR_COLUMNS + 1])
             nc.scalar.mul(out=neg_means[g][:, VECTOR_COLUMNS:], in_=row_sum[:], mul=-1.0 / C_IN)
-            if g > 0:
-                finish_vector_statistics(g - 1)
+
+        def scalar_deviations(g):
+            stds[g] = stat_pool.tile([P, GROUP], F32, name="std")
+            dev_sq = stat_pool.tile([P, GROUP - VECTOR_COLUMNS], F32, name="dev_sq")
             for jj in range(VECTOR_COLUMNS, GROUP):
                 unread = scrap.tile([P, C_IN], BF16, name="unread")
                 nc.scalar.activation(
@@ -183,7 +185,7 @@ def tile_templatepairembeddermultimer_pa_kernel(
                                  start=False, stop=True)
 
         def rank_one(g):
-            res_tiles[g] = work.tile([P, GROUP, P], F32, name="res")
+            res_tiles[g] = res_pool.tile([P, GROUP, P], F32, name="res")
             for m in range(N_FEAT):
                 for jj in range(GROUP):
                     j = g * GROUP + jj
@@ -220,15 +222,17 @@ def tile_templatepairembeddermultimer_pa_kernel(
                 turn_back(s - LAG_TURN_BACK)
             if in_range(s):
                 vector_statistics(s)
-                scalar_statistics(s)
-            if s == N_GROUPS:
-                finish_vector_statistics(N_GROUPS - 1)
+                scalar_sums(s)
             if in_range(s - LAG_TRANSPOSE):
                 gain_shift(s - LAG_TRANSPOSE)
+            if in_range(s):
+                scalar_deviations(s)
             if in_range(s - LAG_PROJECT):
                 copy_out(s - LAG_PROJECT)
-            if in_range(s - LAG_TURN_BACK):
-                rank_one(s - LAG_TURN_BACK)
+            if in_range(s):
+                finish_vector_statistics(s)
+            if in_range(s - LAG_RANK_ONE):
+                rank_one(s - LAG_RANK_ONE)
 
         eps = keep.tile([P, 1], F32, name="eps")
         nc.vector.memset(eps[:], LN_EPS)
@@ -263,6 +267,7 @@ def tile_templatepairembeddermultimer_pa_kernel(
 
         for s in range(LAG_TRANSPOSE):
             step(s)
+        next_step = LAG_TRANSPOSE
 
         columns = keep.tile([P, N_ROWS], F32, name="columns")
         bias_total = keep.tile([P, 1], F32, name="bias_total")
@@ -279,6 +284,10 @@ def tile_templatepairembeddermultimer_pa_kernel(
             rows_t = psum_setup.tile([P, P], BF16, name="rows_t")
             nc.tensor.transpose(rows_t[:], rows[:], ident_b[:])
             nc.vector.tensor_copy(out=columns[:], in_=rows_t[:, 0:N_ROWS])
+
+            step(next_step)
+            next_step += 1
+
             for m in range(4):
                 spread(spread_a[:, m, :], ROW_W + m)
             spread(spread_b[:, 0, :], ROW_W + 4)
@@ -317,5 +326,5 @@ def tile_templatepairembeddermultimer_pa_kernel(
         psum_mx = stack.enter_context(tc.psum_pool(name="psum_mx", bufs=1))
         psum_base = stack.enter_context(tc.psum_pool(name="psum_base", bufs=1))
 
-        for s in range(LAG_TRANSPOSE, N_STEPS):
+        for s in range(next_step, N_STEPS):
             step(s)

@@ -70,6 +70,7 @@ def tile_templatepairembeddermultimer_pa_kernel(
         x_tiles, act_tiles, vector_stats, neg_means, stds, rstds, y_tiles, y_banks, plane_tiles = (
             {}, {}, {}, {}, {}, {}, {}, {}, {})
         grouped_tiles, code_tiles, proj_banks, proj_tiles, res_tiles, bases = {}, {}, {}, {}, {}, {}
+        row_sums, dev_sqs = {}, {}
 
         def columns_of(g):
             return slice(g * GROUP, (g + 1) * GROUP)
@@ -82,35 +83,39 @@ def tile_templatepairembeddermultimer_pa_kernel(
             act_tiles[g] = act_pool.tile([P, GROUP, P], BF16, name="act_g")
             nc.sync.dma_start(out=act_tiles[g][:], in_=act_dgram[:, columns_of(g), :])
 
+
         def vector_statistics(g):
             vector_stats[g] = stat_pool.tile([P, VECTOR_COLUMNS, 2], F32, name="mean_var")
+            partial = stat_pool.tile([P, VECTOR_COLUMNS, 6], F32, name="partial")
             for jj in range(VECTOR_COLUMNS):
-                partial = stat_pool.tile([P, 6], F32, name="partial")
-                nc.vector.bn_stats(out=partial[:], in_=x_tiles[g][:, jj, :])
-                nc.vector.bn_aggr(out=vector_stats[g][:, jj, :], in_=partial[:])
+                nc.vector.bn_stats(out=partial[:, jj, :], in_=x_tiles[g][:, jj, :])
+            for jj in range(VECTOR_COLUMNS):
+                nc.vector.bn_aggr(out=vector_stats[g][:, jj, :], in_=partial[:, jj, :])
 
         def scalar_sums(g):
-            neg_means[g] = stat_pool.tile([P, GROUP], F32, name="neg_mean")
-            row_sum = stat_pool.tile([P, GROUP - VECTOR_COLUMNS], F32, name="row_sum")
+            row_sums[g] = stat_pool.tile([P, GROUP - VECTOR_COLUMNS], F32, name="row_sum")
             for jj in range(VECTOR_COLUMNS, GROUP):
                 unread = scrap.tile([P, C_IN], BF16, name="unread")
                 nc.scalar.activation(
                     out=unread[:], in_=x_tiles[g][:, jj, :], func=ACT.Identity,
-                    accum_out=row_sum[:, jj - VECTOR_COLUMNS : jj - VECTOR_COLUMNS + 1])
-            nc.scalar.mul(out=neg_means[g][:, VECTOR_COLUMNS:], in_=row_sum[:], mul=-1.0 / C_IN)
+                    accum_out=row_sums[g][:, jj - VECTOR_COLUMNS : jj - VECTOR_COLUMNS + 1])
+
+        def scalar_means(g):
+            neg_means[g] = stat_pool.tile([P, GROUP], F32, name="neg_mean")
+            nc.scalar.mul(out=neg_means[g][:, VECTOR_COLUMNS:], in_=row_sums[g][:], mul=-1.0 / C_IN)
 
         def scalar_deviations(g):
-            stds[g] = stat_pool.tile([P, GROUP], F32, name="std")
-            dev_sq = stat_pool.tile([P, GROUP - VECTOR_COLUMNS], F32, name="dev_sq")
+            dev_sqs[g] = stat_pool.tile([P, GROUP - VECTOR_COLUMNS], F32, name="dev_sq")
             for jj in range(VECTOR_COLUMNS, GROUP):
                 unread = scrap.tile([P, C_IN], BF16, name="unread")
                 nc.scalar.activation(
                     out=unread[:], in_=x_tiles[g][:, jj, :], func=ACT.Square, bias=neg_means[g][:, jj : jj + 1],
-                    scale=1.0, accum_out=dev_sq[:, jj - VECTOR_COLUMNS : jj - VECTOR_COLUMNS + 1])
-            nc.scalar.activation(
-                out=stds[g][:, VECTOR_COLUMNS:], in_=dev_sq[:], func=ACT.Sqrt, bias=eps[:, 0:1], scale=1.0 / C_IN)
+                    scale=1.0, accum_out=dev_sqs[g][:, jj - VECTOR_COLUMNS : jj - VECTOR_COLUMNS + 1])
 
-        def finish_vector_statistics(g):
+        def finish_statistics(g):
+            stds[g] = stat_pool.tile([P, GROUP], F32, name="std")
+            nc.scalar.activation(
+                out=stds[g][:, VECTOR_COLUMNS:], in_=dev_sqs[g][:], func=ACT.Sqrt, bias=eps[:, 0:1], scale=1.0 / C_IN)
             nc.scalar.mul(out=neg_means[g][:, 0:VECTOR_COLUMNS], in_=vector_stats[g][:, :, 0], mul=-1.0)
             nc.scalar.activation(
                 out=stds[g][:, 0:VECTOR_COLUMNS], in_=vector_stats[g][:, :, 1], func=ACT.Sqrt, bias=eps[:, 0:1], scale=1.0)
@@ -205,6 +210,7 @@ def tile_templatepairembeddermultimer_pa_kernel(
                 load_x(s + X_AHEAD)
             if in_range(s):
                 load_act(s)
+                scalar_sums(s)
             if in_range(s - LAG_PROJECT):
                 quantise(s - LAG_PROJECT)
             if in_range(s - LAG_STORE):
@@ -222,7 +228,7 @@ def tile_templatepairembeddermultimer_pa_kernel(
                 turn_back(s - LAG_TURN_BACK)
             if in_range(s):
                 vector_statistics(s)
-                scalar_sums(s)
+                scalar_means(s)
             if in_range(s - LAG_TRANSPOSE):
                 gain_shift(s - LAG_TRANSPOSE)
             if in_range(s):
@@ -230,7 +236,7 @@ def tile_templatepairembeddermultimer_pa_kernel(
             if in_range(s - LAG_PROJECT):
                 copy_out(s - LAG_PROJECT)
             if in_range(s):
-                finish_vector_statistics(s)
+                finish_statistics(s)
             if in_range(s - LAG_RANK_ONE):
                 rank_one(s - LAG_RANK_ONE)
 

from contextlib import ExitStack

import concourse.mybir as mybir
from concourse.masks import make_identity

F32 = mybir.dt.float32
BF16 = mybir.dt.bfloat16
U32 = mybir.dt.uint32
U8 = mybir.dt.uint8
FP8X4 = mybir.dt.float8_e4m3fn_x4
ALU = mybir.AluOpType
ACT = mybir.ActivationFunctionType

P = 128
C_IN = 512
PACK = 4
LN_EPS = 1e-5
GROUP = 4
PAIRS = GROUP * P
N_GROUPS = P // GROUP
N_FEAT = 5
X_AHEAD = 4
VECTOR_COLUMNS = 2
GPSIMD_PAIRS = 3 * PAIRS // 4

ROW_GAIN = 0
ROW_SHIFT = 4
ROW_W = 8
ROW_PBM = 13
ROW_BBM = 14
ROW_BIAS = 15
N_ROWS = 21

LAG_NORMALISE = 1
LAG_TRANSPOSE = 2
LAG_REGROUP = 3
LAG_PROJECT = 4
LAG_TURN_BACK = 5
LAG_STORE = 6
LAG_RANK_ONE = 3
N_STEPS = N_GROUPS + LAG_STORE

FLOPS = 2 * P * P * C_IN * P


def as_row(vector):
    return vector.rearrange("(o c) -> o c", o=1)


def tile_templatepairembeddermultimer_pa_kernel(
    tc,
    act_dgram, aa_proj1, aa_proj2, esm_proj1, esm_proj2, query_embedding,
    pseudo_beta_mask, backbone_mask, multichain_mask_2d, unit_x, unit_y, unit_z,
    ln_g, ln_b, w_q, b_q, w_pbm, b_pbm, w_x, b_x, w_y, b_y, w_z, b_z, w_bb, b_bb,
    out,
):
    nc = tc.nc
    with ExitStack() as stack:
        stack.enter_context(tc.manual_schedule())
        keep = stack.enter_context(tc.tile_pool(name="keep", bufs=1))
        x_pool = stack.enter_context(tc.tile_pool(name="x", bufs=X_AHEAD + LAG_NORMALISE + 1))
        act_pool = stack.enter_context(tc.tile_pool(name="act", bufs=LAG_RANK_ONE + 2))
        stat_pool = stack.enter_context(tc.tile_pool(name="stat", bufs=4))
        work = stack.enter_context(tc.tile_pool(name="work", bufs=3))
        scrap = stack.enter_context(tc.tile_pool(name="scrap", bufs=4))
        res_pool = stack.enter_context(tc.tile_pool(name="res", bufs=LAG_STORE - LAG_RANK_ONE + 2))
        psum_keep = stack.enter_context(tc.psum_pool(name="psum_keep", bufs=1))
        psum_y = stack.enter_context(tc.psum_pool(name="psum_y", bufs=PACK))

        x_tiles, act_tiles, vector_stats, neg_means, stds, rstds, y_tiles, y_banks, plane_tiles = (
            {}, {}, {}, {}, {}, {}, {}, {}, {})
        grouped_tiles, code_tiles, proj_banks, proj_tiles, res_tiles, bases = {}, {}, {}, {}, {}, {}
        row_sums, dev_sqs = {}, {}

        def columns_of(g):
            return slice(g * GROUP, (g + 1) * GROUP)

        def load_x(g):
            x_tiles[g] = x_pool.tile([P, GROUP, C_IN], BF16, name="x_g")
            nc.sync.dma_start(out=x_tiles[g][:], in_=query_embedding[:, columns_of(g), :])

        def load_act(g):
            act_tiles[g] = act_pool.tile([P, GROUP, P], BF16, name="act_g")
            nc.sync.dma_start(out=act_tiles[g][:], in_=act_dgram[:, columns_of(g), :])


        def vector_statistics(g):
            vector_stats[g] = stat_pool.tile([P, VECTOR_COLUMNS, 2], F32, name="mean_var")
            partial = stat_pool.tile([P, VECTOR_COLUMNS, 6], F32, name="partial")
            for jj in range(VECTOR_COLUMNS):
                nc.vector.bn_stats(out=partial[:, jj, :], in_=x_tiles[g][:, jj, :])
            for jj in range(VECTOR_COLUMNS):
                nc.vector.bn_aggr(out=vector_stats[g][:, jj, :], in_=partial[:, jj, :])

        def scalar_sums(g):
            row_sums[g] = stat_pool.tile([P, GROUP - VECTOR_COLUMNS], F32, name="row_sum")
            for jj in range(VECTOR_COLUMNS, GROUP):
                unread = scrap.tile([P, C_IN], BF16, name="unread")
                nc.scalar.activation(
                    out=unread[:], in_=x_tiles[g][:, jj, :], func=ACT.Identity,
                    accum_out=row_sums[g][:, jj - VECTOR_COLUMNS : jj - VECTOR_COLUMNS + 1])

        def scalar_means(g):
            neg_means[g] = stat_pool.tile([P, GROUP], F32, name="neg_mean")
            nc.scalar.mul(out=neg_means[g][:, VECTOR_COLUMNS:], in_=row_sums[g][:], mul=-1.0 / C_IN)

        def scalar_deviations(g):
            dev_sqs[g] = stat_pool.tile([P, GROUP - VECTOR_COLUMNS], F32, name="dev_sq")
            for jj in range(VECTOR_COLUMNS, GROUP):
                unread = scrap.tile([P, C_IN], BF16, name="unread")
                nc.scalar.activation(
                    out=unread[:], in_=x_tiles[g][:, jj, :], func=ACT.Square, bias=neg_means[g][:, jj : jj + 1],
                    scale=1.0, accum_out=dev_sqs[g][:, jj - VECTOR_COLUMNS : jj - VECTOR_COLUMNS + 1])

        def finish_statistics(g):
            stds[g] = stat_pool.tile([P, GROUP], F32, name="std")
            nc.scalar.activation(
                out=stds[g][:, VECTOR_COLUMNS:], in_=dev_sqs[g][:], func=ACT.Sqrt, bias=eps[:, 0:1], scale=1.0 / C_IN)
            nc.scalar.mul(out=neg_means[g][:, 0:VECTOR_COLUMNS], in_=vector_stats[g][:, :, 0], mul=-1.0)
            nc.scalar.activation(
                out=stds[g][:, 0:VECTOR_COLUMNS], in_=vector_stats[g][:, :, 1], func=ACT.Sqrt, bias=eps[:, 0:1], scale=1.0)

        def inverse_std(g):
            rstds[g] = stat_pool.tile([P, GROUP], F32, name="rstd")
            nc.vector.reciprocal(out=rstds[g][:], in_=stds[g][:])

        def normalise(g):
            y_tiles[g] = work.tile([P, GROUP, C_IN], F32, name="y_g")
            for jj in range(GROUP):
                nc.gpsimd.tensor_scalar(
                    out=y_tiles[g][:, jj, :], in0=x_tiles[g][:, jj, :],
                    scalar1=neg_means[g][:, jj : jj + 1], scalar2=rstds[g][:, jj : jj + 1], op0=ALU.add, op1=ALU.mult)

        def transpose(g):
            y_banks[g] = []
            for t in range(PACK):
                y_t = psum_y.tile([P, GROUP, P], F32, name="y_t")
                for jj in range(GROUP):
                    nc.tensor.transpose(y_t[:, jj, :], y_tiles[g][:, jj, t * P : (t + 1) * P], ident_f[:])
                y_banks[g].append(y_t)

        def gain_shift(g):
            plane_tiles[g] = work.tile([P, PACK, PAIRS], BF16, name="q_planes")
            for t in range(PACK):
                nc.scalar.activation(
                    out=plane_tiles[g][:, t, :], in_=y_banks[g][t][:].rearrange("p a b -> p (a b)"), func=ACT.Identity,
                    scale=columns[:, ROW_GAIN + t : ROW_GAIN + t + 1], bias=columns[:, ROW_SHIFT + t : ROW_SHIFT + t + 1])

        def regroup(g):
            q_planes = plane_tiles[g]
            q_grouped = work.tile([P, PAIRS, PACK], BF16, name="q_grouped", align_bytes=64)
            grouped_tiles[g] = q_grouped
            nc.gpsimd.tensor_scalar(
                out=q_grouped[:, 0:GPSIMD_PAIRS, :], in0=q_planes[:, :, 0:GPSIMD_PAIRS].rearrange("p t r -> p r t"),
                scalar1=1.0, scalar2=0.0, op0=ALU.mult, op1=ALU.add)
            nc.scalar.copy(
                out=q_grouped[:, GPSIMD_PAIRS:, :].rearrange("p (c i) t -> p c t i", i=4),
                in_=q_planes[:, :, GPSIMD_PAIRS:].rearrange("p t (c i) -> p c t i", i=4))

        def quantise(g):
            q_codes = work.tile([P, PAIRS], U32, name="q_codes", align_bytes=64)
            q_scales = work.tile([P, PAIRS], U8, name="q_scales", align_bytes=64)
            nc.vector.quantize_mx(
                out=q_codes[:].bitcast(FP8X4), scales=q_scales[:], in_=grouped_tiles[g][:].rearrange("p r t -> p (r t)"))
            code_tiles[g] = (q_codes, q_scales)

        def project(g):
            q_codes, q_scales = code_tiles[g]
            proj_banks[g] = psum_mx.tile([P, PAIRS], F32, name="proj_ps")
            nc.tensor.matmul_mx(
                out=proj_banks[g][:],
                lhsT=w_codes[:].bitcast(FP8X4), lhsT_scale=w_scales[:],
                rhs=q_codes[:].bitcast(FP8X4), rhs_scale=q_scales[:],
                start=True, stop=True)

        def copy_out(g):
            proj_tiles[g] = work.tile([P, GROUP, P], F32, name="proj_t")
            nc.scalar.copy(out=proj_tiles[g][:].rearrange("p a b -> p (a b)"), in_=proj_banks[g][:])

        def turn_back(g):
            base = psum_base.tile([P, GROUP, P], F32, name="base")
            bases[g] = base
            for jj in range(GROUP):
                j = g * GROUP + jj
                nc.tensor.matmul(out=base[:, jj, :], lhsT=col_term_t[:], rhs=ident_f[:], is_transpose=True,
                                 start=True, stop=False)
                nc.tensor.matmul(out=base[:, jj, :], lhsT=row_term_t[:, j : j + 1].to_broadcast([P, P]), rhs=ident_f[:],
                                 is_transpose=True, start=False, stop=False)
                nc.tensor.matmul(out=base[:, jj, :], lhsT=proj_tiles[g][:, jj, :], rhs=ident_f[:], is_transpose=True,
                                 start=False, stop=True)

        def rank_one(g):
            res_tiles[g] = res_pool.tile([P, GROUP, P], F32, name="res")
            for m in range(N_FEAT):
                for jj in range(GROUP):
                    j = g * GROUP + jj
                    nc.vector.scalar_tensor_tensor(
                        out=res_tiles[g][:, jj, :], in0=w_spread[m], scalar=feat[:, m, j : j + 1],
                        in1=act_tiles[g][:, jj, :] if m == 0 else res_tiles[g][:, jj, :], op0=ALU.mult, op1=ALU.add)

        def add_store(g):
            nc.vector.tensor_tensor(out=res_tiles[g][:], in0=res_tiles[g][:], in1=bases[g][:], op=ALU.add)
            nc.sync.dma_start(out=out[:, columns_of(g), :], in_=res_tiles[g][:])

        def in_range(g):
            return 0 <= g < N_GROUPS

        def step(s):
            if in_range(s + X_AHEAD):
                load_x(s + X_AHEAD)
            if in_range(s):
                load_act(s)
                scalar_sums(s)
            if in_range(s - LAG_PROJECT):
                quantise(s - LAG_PROJECT)
            if in_range(s - LAG_STORE):
                add_store(s - LAG_STORE)
            if in_range(s - LAG_REGROUP):
                regroup(s - LAG_REGROUP)
            if in_range(s - LAG_NORMALISE):
                inverse_std(s - LAG_NORMALISE)
                normalise(s - LAG_NORMALISE)
            if in_range(s - LAG_TRANSPOSE):
                transpose(s - LAG_TRANSPOSE)
            if in_range(s - LAG_PROJECT):
                project(s - LAG_PROJECT)
            if in_range(s - LAG_TURN_BACK):
                turn_back(s - LAG_TURN_BACK)
            if in_range(s):
                vector_statistics(s)
                scalar_means(s)
            if in_range(s - LAG_TRANSPOSE):
                gain_shift(s - LAG_TRANSPOSE)
            if in_range(s):
                scalar_deviations(s)
            if in_range(s - LAG_PROJECT):
                copy_out(s - LAG_PROJECT)
            if in_range(s):
                finish_statistics(s)
            if in_range(s - LAG_RANK_ONE):
                rank_one(s - LAG_RANK_ONE)

        eps = keep.tile([P, 1], F32, name="eps")
        nc.vector.memset(eps[:], LN_EPS)
        rows = keep.tile([P, P], BF16, name="rows")
        nc.vector.memset(rows[:], 0.0)
        table_warm = keep.tile([P, 1], F32, name="table_warm")
        nc.scalar.activation(out=table_warm[:], in_=eps[:], func=ACT.Sqrt)
        ident_f = keep.tile([P, P], F32, name="ident_f")
        make_identity(nc, ident_f[:])
        ident_b = keep.tile([P, P], BF16, name="ident_b")
        make_identity(nc, ident_b[:])

        load_x(0)
        load_x(1)
        nc.sync.dma_start(out=rows[ROW_GAIN : ROW_GAIN + PACK, :], in_=ln_g.rearrange("(t p) -> t p", p=P))
        nc.sync.dma_start(out=rows[ROW_SHIFT : ROW_SHIFT + PACK, :], in_=ln_b.rearrange("(t p) -> t p", p=P))
        for n, row in enumerate((w_pbm, w_x, w_y, w_z, w_bb, as_row(pseudo_beta_mask), as_row(backbone_mask))):
            nc.sync.dma_start(out=rows[ROW_W + n : ROW_W + n + 1, :], in_=row)
        load_x(2)
        for n, vector in enumerate((b_q, b_pbm, b_x, b_y, b_z, b_bb)):
            nc.sync.dma_start(out=rows[ROW_BIAS + n : ROW_BIAS + n + 1, :], in_=as_row(vector))
        w_planes = keep.tile([P, PACK, P], BF16, name="w_planes")
        nc.sync.dma_start(out=w_planes[:], in_=w_q.rearrange("(t p) c -> p t c", p=P))
        load_x(3)
        small = {}
        for name, matrix in (
            ("mc", multichain_mask_2d), ("ux", unit_x), ("uy", unit_y), ("uz", unit_z),
            ("aa1", aa_proj1), ("esm1", esm_proj1), ("aa2", aa_proj2), ("esm2", esm_proj2),
        ):
            small[name] = keep.tile([P, P], BF16, name="in_" + name)
            nc.sync.dma_start(out=small[name][:], in_=matrix)

        for s in range(LAG_TRANSPOSE):
            step(s)
        next_step = LAG_TRANSPOSE

        columns = keep.tile([P, N_ROWS], F32, name="columns")
        bias_total = keep.tile([P, 1], F32, name="bias_total")
        row_term_t = keep.tile([P, P], F32, name="row_term_t")
        col_term_t = keep.tile([P, P], F32, name="col_term_t")
        feat = keep.tile([P, N_FEAT, P], F32, name="feat")
        spread_a = psum_keep.tile([P, 4, P], F32, name="spread_a")
        spread_b = psum_keep.tile([P, 3, P], F32, name="spread_b")

        def spread(dst, row):
            nc.tensor.transpose(dst, columns[:, row : row + 1].to_broadcast([P, P]), ident_f[:])

        with tc.psum_pool(name="psum_setup", bufs=1) as psum_setup:
            rows_t = psum_setup.tile([P, P], BF16, name="rows_t")
            nc.tensor.transpose(rows_t[:], rows[:], ident_b[:])
            nc.vector.tensor_copy(out=columns[:], in_=rows_t[:, 0:N_ROWS])

            step(next_step)
            next_step += 1

            for m in range(4):
                spread(spread_a[:, m, :], ROW_W + m)
            spread(spread_b[:, 0, :], ROW_W + 4)
            spread(spread_b[:, 1, :], ROW_PBM)
            spread(spread_b[:, 2, :], ROW_BBM)
            w_spread = [spread_a[:, m, :] for m in range(4)] + [spread_b[:, 0, :]]
            nc.vector.reduce_sum(out=bias_total[:], in_=columns[:, ROW_BIAS:N_ROWS], axis=mybir.AxisListType.X)

            w_grouped = keep.tile([P, P, PACK], BF16, name="w_grouped", align_bytes=64)
            nc.vector.tensor_copy(out=w_grouped[:], in_=w_planes[:].rearrange("p t c -> p c t"))
            w_codes = keep.tile([P, P], U32, name="w_codes", align_bytes=64)
            w_scales = keep.tile([P, P], U8, name="w_scales", align_bytes=64)
            nc.vector.quantize_mx(
                out=w_codes[:].bitcast(FP8X4), scales=w_scales[:], in_=w_grouped[:].rearrange("p c t -> p (c t)"))

            nc.vector.scalar_tensor_tensor(
                out=feat[:, 0, :], in0=small["mc"][:], scalar=columns[:, ROW_PBM : ROW_PBM + 1], in1=spread_b[:, 1, :],
                op0=ALU.mult, op1=ALU.mult)
            nc.vector.scalar_tensor_tensor(
                out=feat[:, 4, :], in0=small["mc"][:], scalar=columns[:, ROW_BBM : ROW_BBM + 1], in1=spread_b[:, 2, :],
                op0=ALU.mult, op1=ALU.mult)
            for m, name in ((1, "ux"), (2, "uy"), (3, "uz")):
                nc.vector.tensor_tensor(out=feat[:, m, :], in0=small[name][:], in1=feat[:, 4, :], op=ALU.mult)

            row_term = keep.tile([P, P], F32, name="row_term")
            nc.vector.tensor_tensor(out=row_term[:], in0=small["aa1"][:], in1=small["esm1"][:], op=ALU.add)
            col_term = keep.tile([P, P], F32, name="col_term")
            nc.vector.tensor_tensor(out=col_term[:], in0=small["aa2"][:], in1=small["esm2"][:], op=ALU.add)
            term_bank = psum_setup.tile([P, 2, P], F32, name="term_bank")
            nc.tensor.transpose(term_bank[:, 0, :], row_term[:], ident_f[:])
            nc.tensor.transpose(term_bank[:, 1, :], col_term[:], ident_f[:])
            nc.vector.tensor_copy(out=row_term_t[:], in_=term_bank[:, 0, :])
            nc.vector.tensor_scalar(
                out=col_term_t[:], in0=term_bank[:, 1, :], scalar1=bias_total[:, 0:1], scalar2=None, op0=ALU.add)

        psum_mx = stack.enter_context(tc.psum_pool(name="psum_mx", bufs=1))
        psum_base = stack.enter_context(tc.psum_pool(name="psum_base", bufs=1))

        for s in range(next_step, N_STEPS):
            step(s)
